import numpy as np
import ml_dtypes


def mxq(x, axis, fmt="e4m3"):
    dtype, down = {"e4m3": (ml_dtypes.float8_e4m3fn, 7), "e5m2": (ml_dtypes.float8_e5m2, 14)}[fmt]
    v = np.moveaxis(np.asarray(x, np.float32).astype(ml_dtypes.bfloat16).astype(np.float64), axis, -1)
    blocks = v.reshape(v.shape[:-1] + (-1, 32))
    amax = np.abs(blocks).max(-1, keepdims=True)
    byte = np.maximum(np.where(amax > 0, np.frexp(amax)[1] - 1 + 127, 0) - down, 1)
    scale = np.exp2(byte - 127.0)
    codes = (blocks / scale).astype(np.float32).astype(dtype).astype(np.float64)
    return np.moveaxis((codes * scale).reshape(v.shape), -1, axis)


WIDE = False


def mx_kscale(k):
    if not WIDE:
        return np.ones(k)
    levels = np.array([10, -10, 5, -5, 0])
    a = np.random.permutation(np.resize(levels, k // 512 * 4)).reshape(k // 512, 4)
    idx = np.arange(k)
    return np.exp2(a[idx // 512, idx % 128 // 32])


BF16 = ml_dtypes.bfloat16


def bf(x):
    return np.asarray(x, np.float32).astype(BF16)


def f64(x):
    return np.asarray(x).astype(np.float64)


N, D = 512, 512
C_IN = 1.0
C_OUT = 1.0
EPS = 1e-15
BOUND = 1.0 - 168.0 * 2.0 ** -24
LN_EPS = 1e-5


def atanh(z):
    return 0.5 * np.log((1.0 + z) / (1.0 - z))


def _norm(x):
    return np.clip(np.linalg.norm(x, axis=-1, keepdims=True), EPS, None)


def logmap0(x, c):
    sc = c ** 0.5
    n = _norm(x)
    return atanh(np.clip(sc * n, None, BOUND)) * x / (sc * n)


def expmap0(u, c):
    sc = c ** 0.5
    n = _norm(u)
    return np.tanh(sc * n) * u / (sc * n)


def mobius_add(x, y, c):
    x2 = np.sum(x * x, -1, keepdims=True)
    y2 = np.sum(y * y, -1, keepdims=True)
    xy = np.sum(x * y, -1, keepdims=True)
    num = (1.0 + 2.0 * c * xy + c * y2) * x + (1.0 - c * x2) * y
    den = 1.0 + 2.0 * c * xy + (c * c) * x2 * y2
    return num / np.clip(den, EPS, None)


def expmap(x, u, c):
    sc = c ** 0.5
    n = _norm(u)
    lam = 2.0 / np.clip(1.0 - c * np.sum(x * x, -1, keepdims=True), EPS, None)
    second = np.tanh(sc * lam * n / 2.0) * u / (sc * n)
    return mobius_add(x, second, c)


def transp0(y, v, c):
    return v * (1.0 - c * np.sum(y * y, -1, keepdims=True))


def setup_inputs():
    s = mx_kscale(D)
    s = s / np.sqrt(np.mean(s * s))
    c = np.random.uniform(0.5, 0.8, (N, 1))
    far = np.random.uniform(0.0, 1.0, (N, 1)) < 0.5
    tau = np.where(far, np.random.uniform(1.5, 2.0, (N, 1)), np.exp(np.random.uniform(np.log(0.04), np.log(0.1), (N, 1))))
    h = c / np.sqrt(D) + tau * np.sqrt(LN_EPS) * np.random.standard_normal((N, D))
    gamma = 12.0 / np.sqrt(D) * (1.0 + 0.1 * np.random.standard_normal(D)) * s
    beta = 0.8 / np.sqrt(D) * np.random.standard_normal(D) * s
    weight = 0.25 / np.sqrt(D) * np.random.standard_normal((D, D)) / s[None, :]
    bias = 0.4 / np.sqrt(D) * np.random.standard_normal((1, D))
    return {'h': bf(h), 'weight': bf(weight), 'bias': bf(bias), 'gamma': bf(gamma), 'beta': bf(beta)}


def reference(h, weight, bias, gamma, beta):
    x = logmap0(f64(h), C_IN)
    mu = np.mean(x, -1, keepdims=True)
    var = np.mean((x - mu) ** 2, -1, keepdims=True)
    x = (x - mu) * (1.0 / np.sqrt(var + LN_EPS)) * f64(gamma) + f64(beta)
    hn = expmap0(x, C_IN)
    u = logmap0(hn, C_IN)
    xt = mxq(u, 1, 'e4m3') @ mxq(f64(weight), 1, 'e4m3').T
    res = expmap0(xt, C_IN)
    b = transp0(res, f64(bias), C_IN)
    res = expmap(res, b, C_IN)
    return expmap0(np.maximum(logmap0(res, C_IN), 0.0), C_OUT)

@@ -1,0 +1,411 @@
+import math
+from contextlib import ExitStack
+
+import concourse.mybir as mybir
+from concourse.masks import make_identity
+
+F32 = mybir.dt.float32
+BF16 = mybir.dt.bfloat16
+U32 = mybir.dt.uint32
+U8 = mybir.dt.uint8
+FP8X4 = mybir.dt.float8_e4m3fn_x4
+ALU = mybir.AluOpType
+ACT = mybir.ActivationFunctionType
+
+P = 128
+PACK = 4
+N_ROWS = 512
+D = 512
+TILES = N_ROWS // P
+
+BOUND = 1.0 - 168.0 * 2.0 ** -24
+ARTANH_BOUND = 0.5 * math.log((1.0 + BOUND) / (1.0 - BOUND))
+LN_EPS = 1e-5
+NORM_MIN = 1e-15
+NORM_MIN_SQ = 1e-30
+
+FLOPS = 2 * N_ROWS * D * D
+
+
+def tile_hnnlayer_s_kernel(tc, h, weight, bias, gamma, beta, out):
+    nc = tc.nc
+    with ExitStack() as ctx:
+        keep = ctx.enter_context(tc.tile_pool(name="keep", bufs=1))
+        scrap = ctx.enter_context(tc.tile_pool(name="scrap", bufs=4))
+        psum_tr = ctx.enter_context(tc.psum_pool(name="psum_tr", bufs=4))
+        psum_xt = ctx.enter_context(tc.psum_pool(name="psum_xt", bufs=1))
+        ctx.enter_context(tc.manual_schedule())
+
+        def per_tile(shape, dtype, name):
+            return [
+                keep.tile(shape, dtype, name="%s%d" % (name, i), align_bytes=64)
+                for i in range(TILES)
+            ]
+
+        def row_numbers(name):
+            return keep.tile([P, TILES], F32, name=name)
+
+        def one_number(name):
+            return keep.tile([P, 1], F32, name=name)
+
+        h_sb = per_tile([P, D], BF16, "h_sb")
+        for i in range(TILES):
+            nc.sync.dma_start(out=h_sb[i][:], in_=h[i * P : (i + 1) * P, :])
+        gamma_bc = keep.tile([P, D], BF16, name="gamma_bc")
+        nc.sync.dma_start(out=gamma_bc[:], in_=gamma.partition_broadcast(P))
+        bias_bc = keep.tile([P, D], BF16, name="bias_bc")
+        nc.sync.dma_start(
+            out=bias_bc[:], in_=bias.rearrange("o d -> (o d)").partition_broadcast(P)
+        )
+        beta_bc = keep.tile([P, D], BF16, name="beta_bc")
+        nc.sync.dma_start(out=beta_bc[:], in_=beta.partition_broadcast(P))
+        w_sb = keep.tile([P, TILES, D], BF16, name="w_sb")
+        nc.sync.dma_start(out=w_sb[:], in_=weight.rearrange("(o p) k -> p o k", p=P))
+
+        half = row_numbers("half")
+        nc.vector.memset(half[:], 0.5)
+        neg_half = row_numbers("neg_half")
+        nc.vector.memset(neg_half[:], -0.5)
+        ones = one_number("ones")
+        nc.vector.memset(ones[:], 1.0)
+        ident = keep.tile([P, P], BF16, name="ident")
+        make_identity(nc, ident[:])
+
+        def load_table(func, name):
+            unused = one_number(name)
+            nc.scalar.activation(out=unused[:], in_=ones[:], func=func)
+
+        def square_sum(src, total):
+            squares = scrap.tile([P, D], BF16, name="squares")
+            nc.scalar.activation(out=squares[:], in_=src, func=ACT.Square, accum_out=total)
+
+        load_table(ACT.Ln, "warm_ln_a")
+
+        first = row_numbers("first")
+        d = per_tile([P, D], F32, "d")
+        d_sum = row_numbers("d_sum")
+        d_sq = row_numbers("d_sq")
+        for i in range(TILES):
+            squares = scrap.tile([P, D], BF16, name="squares")
+            nc.scalar.activation(
+                out=squares[:], in_=h_sb[i][:], func=ACT.Square, scale=-1.0,
+                bias=h_sb[i][:, 0:1], accum_out=d_sq[:, i : i + 1],
+            )
+            nc.vector.tensor_scalar(
+                out=d[i][:], in0=h_sb[i][:], scalar1=h_sb[i][:, 0:1], scalar2=None,
+                op0=ALU.subtract, op1=ALU.add, accum_out=d_sum[:, i : i + 1],
+            )
+            nc.vector.tensor_copy(out=first[:, i : i + 1], in_=h_sb[i][:, 0:1])
+        h_sq_a = row_numbers("h_sq_a")
+        nc.vector.scalar_tensor_tensor(
+            out=h_sq_a[:], in0=first[:], scalar=0.5 * D, in1=d_sum[:], op0=ALU.mult, op1=ALU.add
+        )
+        h_sq_b = row_numbers("h_sq_b")
+        nc.vector.scalar_tensor_tensor(
+            out=h_sq_b[:], in0=h_sq_a[:], scalar=2.0, in1=first[:], op0=ALU.mult, op1=ALU.mult
+        )
+        h_sq = row_numbers("h_sq")
+        nc.vector.tensor_add(out=h_sq[:], in0=h_sq_b[:], in1=d_sq[:])
+
+        centred = per_tile([P, D], F32, "centred")
+        d_mean = row_numbers("d_mean")
+
+        def centre(i):
+            nc.vector.scalar_tensor_tensor(
+                out=centred[i][:], in0=d[i][:], scalar=d_mean[:, i : i + 1],
+                in1=gamma_bc[:], op0=ALU.subtract, op1=ALU.mult,
+            )
+
+        h_norm = row_numbers("h_norm")
+        nc.gpsimd.tensor_tensor(out=h_norm[:], in0=h_sq[:], in1=half[:], op=ALU.pow)
+        h_clip = row_numbers("h_clip")
+        nc.gpsimd.tensor_scalar_min(out=h_clip[:], in0=h_norm[:], scalar1=BOUND)
+        nc.vector.tensor_scalar_mul(out=d_mean[:], in0=d_sum[:], scalar1=1.0 / D)
+        centre(0)
+        centre(1)
+        d_sum_mean = row_numbers("d_sum_mean")
+        nc.vector.tensor_mul(out=d_sum_mean[:], in0=d_sum[:], in1=d_mean[:])
+        dev_sq = row_numbers("dev_sq")
+        nc.vector.tensor_sub(out=dev_sq[:], in0=d_sq[:], in1=d_sum_mean[:])
+        eps_h_sq = row_numbers("eps_h_sq")
+        nc.vector.tensor_scalar(
+            out=eps_h_sq[:], in0=h_sq[:], scalar1=NORM_MIN_SQ, scalar2=LN_EPS,
+            op0=ALU.max, op1=ALU.mult,
+        )
+        ln_up = row_numbers("ln_up")
+        nc.scalar.activation(out=ln_up[:], in_=h_clip[:], func=ACT.Ln, bias=1.0, scale=1.0)
+        ln_dn = row_numbers("ln_dn")
+        nc.scalar.activation(out=ln_dn[:], in_=h_clip[:], func=ACT.Ln, bias=1.0, scale=-1.0)
+        centre(2)
+        theta2 = row_numbers("theta2")
+        nc.vector.tensor_sub(out=theta2[:], in0=ln_up[:], in1=ln_dn[:])
+        theta_sq = row_numbers("theta_sq")
+        nc.vector.scalar_tensor_tensor(
+            out=theta_sq[:], in0=theta2[:], scalar=0.25 / D, in1=theta2[:],
+            op0=ALU.mult, op1=ALU.mult,
+        )
+        theta_sq_var = row_numbers("theta_sq_var")
+        nc.vector.tensor_mul(out=theta_sq_var[:], in0=theta_sq[:], in1=dev_sq[:])
+        k_arg = row_numbers("k_arg")
+        nc.vector.tensor_add(out=k_arg[:], in0=theta_sq_var[:], in1=eps_h_sq[:])
+        k_rsqrt = row_numbers("k_rsqrt")
+        nc.gpsimd.tensor_tensor(out=k_rsqrt[:], in0=k_arg[:], in1=neg_half[:], op=ALU.pow)
+        centre(3)
+
+        bias_sq = one_number("bias_sq")
+        square_sum(bias_bc[:], bias_sq[:])
+        load_table(ACT.Tanh, "warm_tanh_a")
+        bias_sq_clip = one_number("bias_sq_clip")
+        nc.vector.tensor_scalar_max(out=bias_sq_clip[:], in0=bias_sq[:], scalar1=NORM_MIN_SQ)
+        bias_norm = one_number("bias_norm")
+        nc.gpsimd.tensor_tensor(
+            out=bias_norm[:], in0=bias_sq_clip[:], in1=half[:, 0:1], op=ALU.pow
+        )
+
+        k = row_numbers("k")
+        nc.vector.scalar_tensor_tensor(
+            out=k[:], in0=theta2[:], scalar=0.5, in1=k_rsqrt[:], op0=ALU.mult, op1=ALU.mult
+        )
+
+        x = per_tile([P, D], F32, "x")
+        x_sq = row_numbers("x_sq")
+        for i in range(TILES):
+            nc.vector.scalar_tensor_tensor(
+                out=x[i][:], in0=centred[i][:], scalar=k[:, i : i + 1], in1=beta_bc[:],
+                op0=ALU.mult, op1=ALU.add,
+            )
+            square_sum(x[i][:], x_sq[:, i : i + 1])
+        x_rnorm = row_numbers("x_rnorm")
+        nc.gpsimd.tensor_tensor(out=x_rnorm[:], in0=x_sq[:], in1=neg_half[:], op=ALU.pow)
+
+        w_grouped = keep.tile([P, D, PACK], BF16, name="w_grouped", align_bytes=64)
+        w_codes = keep.tile([P, D], U32, name="w_codes", align_bytes=64)
+        w_scales = keep.tile([P, D], U8, name="w_scales", align_bytes=64)
+        w_t = []
+        for pair in range(2):
+            w_t.append(psum_tr.tile([P, 2, PACK, P], BF16, name="w_t%d" % pair, tag="tr"))
+            for a in range(2):
+                for t in range(PACK):
+                    nc.tensor.transpose(
+                        out=w_t[pair][:, a, t, :],
+                        in_=w_sb[:, 2 * pair + a, t * P : (t + 1) * P],
+                        identity=ident[:],
+                    )
+        bias_tanh = one_number("bias_tanh")
+        nc.scalar.activation(out=bias_tanh[:], in_=bias_norm[:], func=ACT.Tanh)
+        nc.scalar.copy(
+            out=w_grouped[:, 0 : 2 * P, :].rearrange("p (a r) t -> p a r t", a=2),
+            in_=w_t[0][:].rearrange("p a t r -> p a r t"),
+        )
+        nc.vector.tensor_copy(
+            out=w_grouped[:, 2 * P : 4 * P, :].rearrange("p (a r) t -> p a r t", a=2),
+            in_=w_t[1][:].rearrange("p a t r -> p a r t"),
+        )
+
+        bias_rnorm = one_number("bias_rnorm")
+        nc.vector.reciprocal(out=bias_rnorm[:], in_=bias_norm[:])
+        y_scale = one_number("y_scale")
+        nc.vector.tensor_mul(out=y_scale[:], in0=bias_tanh[:], in1=bias_rnorm[:])
+        neg_y_scale = one_number("neg_y_scale")
+        nc.vector.tensor_scalar_mul(out=neg_y_scale[:], in0=y_scale[:], scalar1=-1.0)
+        y_sq = one_number("y_sq")
+        nc.vector.tensor_scalar(
+            out=y_sq[:], in0=bias_sq[:], scalar1=y_scale[:], scalar2=y_scale[:],
+            op0=ALU.mult, op1=ALU.mult,
+        )
+        one_plus_y_sq = one_number("one_plus_y_sq")
+        nc.vector.tensor_scalar_add(out=one_plus_y_sq[:], in0=y_sq[:], scalar1=1.0)
+
+        shrink = row_numbers("shrink")
+        nc.vector.tensor_scalar(
+            out=shrink[:], in0=x_rnorm[:], scalar1=ARTANH_BOUND, scalar2=1.0,
+            op0=ALU.mult, op1=ALU.min,
+        )
+        nc.vector.quantize_mx(
+            out=w_codes[:].bitcast(FP8X4),
+            scales=w_scales[:],
+            in_=w_grouped[:].rearrange("p c t -> p (c t)"),
+        )
+
+        u = per_tile([P, D], BF16, "u")
+        u_grouped = per_tile([P, P, PACK], BF16, "u_grouped")
+        u_codes = per_tile([P, P], U32, "u_codes")
+        u_scales = per_tile([P, P], U8, "u_scales")
+        xt = [psum_xt.tile([P, D], F32, name="xt%d" % i) for i in range(TILES)]
+        xt_sq = row_numbers("xt_sq")
+        xt_y = row_numbers("xt_y")
+
+        def make_u(i):
+            nc.scalar.activation(
+                out=u[i][:], in_=x[i][:], func=ACT.Copy, scale=shrink[:, i : i + 1]
+            )
+            u_t = psum_tr.tile([P, PACK, P], BF16, name="u_t", tag="tr")
+            for t in range(PACK):
+                nc.tensor.transpose(
+                    out=u_t[:, t, :], in_=u[i][:, t * P : (t + 1) * P], identity=ident[:]
+                )
+            nc.vector.tensor_copy(out=u_grouped[i][:], in_=u_t[:].rearrange("p t r -> p r t"))
+
+        def multiply(i):
+            nc.vector.quantize_mx(
+                out=u_codes[i][:].bitcast(FP8X4),
+                scales=u_scales[i][:],
+                in_=u_grouped[i][:].rearrange("p r t -> p (r t)"),
+            )
+            nc.tensor.matmul_mx(
+                out=xt[i][:],
+                lhsT=u_codes[i][:].bitcast(FP8X4),
+                lhsT_scale=u_scales[i][:],
+                rhs=w_codes[:].bitcast(FP8X4),
+                rhs_scale=w_scales[:],
+                start=True,
+                stop=True,
+            )
+
+        def row_sums(i):
+            square_sum(xt[i][:], xt_sq[:, i : i + 1])
+            products = scrap.tile([P, D], F32, name="products")
+            nc.vector.scalar_tensor_tensor(
+                out=products[:], in0=xt[i][:], scalar=y_scale[:], in1=bias_bc[:],
+                op0=ALU.mult, op1=ALU.mult, accum_out=xt_y[:, i : i + 1],
+            )
+
+        for step in range(TILES + 2):
+            if step < TILES:
+                make_u(step)
+            if 1 <= step <= TILES:
+                multiply(step - 1)
+            if step >= 2:
+                row_sums(step - 2)
+
+        xt_norm = row_numbers("xt_norm")
+        nc.gpsimd.tensor_tensor(out=xt_norm[:], in0=xt_sq[:], in1=half[:], op=ALU.pow)
+        r_norm = row_numbers("r_norm")
+        nc.scalar.activation(out=r_norm[:], in_=xt_norm[:], func=ACT.Tanh)
+        load_table(ACT.Ln, "warm_ln_b")
+        xt_norm_clip = row_numbers("xt_norm_clip")
+        nc.vector.tensor_scalar_max(out=xt_norm_clip[:], in0=xt_norm[:], scalar1=NORM_MIN)
+        xt_rnorm = row_numbers("xt_rnorm")
+        nc.vector.reciprocal(out=xt_rnorm[:], in_=xt_norm_clip[:])
+        xt_y_unit2 = row_numbers("xt_y_unit2")
+        nc.vector.scalar_tensor_tensor(
+            out=xt_y_unit2[:], in0=xt_rnorm[:], scalar=2.0, in1=xt_y[:],
+            op0=ALU.mult, op1=ALU.mult,
+        )
+        r_y2 = row_numbers("r_y2")
+        nc.vector.tensor_mul(out=r_y2[:], in0=r_norm[:], in1=xt_y_unit2[:])
+        rho = row_numbers("rho")
+        nc.vector.tensor_mul(out=rho[:], in0=r_norm[:], in1=xt_rnorm[:])
+        neg_ys_r_sq = row_numbers("neg_ys_r_sq")
+        nc.vector.scalar_tensor_tensor(
+            out=neg_ys_r_sq[:], in0=r_norm[:], scalar=neg_y_scale[:], in1=r_norm[:],
+            op0=ALU.mult, op1=ALU.mult,
+        )
+        xt_coef = row_numbers("xt_coef")
+        nc.vector.scalar_tensor_tensor(
+            out=xt_coef[:], in0=r_y2[:], scalar=one_plus_y_sq[:], in1=rho[:],
+            op0=ALU.add, op1=ALU.mult,
+        )
+        xt_rcoef = row_numbers("xt_rcoef")
+        nc.vector.reciprocal(out=xt_rcoef[:], in_=xt_coef[:])
+        bias_coef = row_numbers("bias_coef")
+        nc.vector.scalar_tensor_tensor(
+            out=bias_coef[:], in0=neg_ys_r_sq[:], scalar=y_scale[:], in1=xt_rcoef[:],
+            op0=ALU.add, op1=ALU.mult,
+        )
+
+        z = per_tile([P, D], F32, "z")
+        relu_sq = row_numbers("relu_sq")
+
+        def direction(i):
+            nc.vector.scalar_tensor_tensor(
+                out=z[i][:], in0=bias_bc[:], scalar=bias_coef[:, i : i + 1], in1=xt[i][:],
+                op0=ALU.mult, op1=ALU.add,
+            )
+
+        def relu_square_sum(i):
+            products = scrap.tile([P, D], F32, name="products")
+            nc.vector.scalar_tensor_tensor(
+                out=products[:], in0=z[i][:], scalar=0.0, in1=z[i][:],
+                op0=ALU.max, op1=ALU.mult, accum_out=relu_sq[:, i : i + 1],
+            )
+
+        direction(0)
+        r_sq = row_numbers("r_sq")
+        nc.vector.tensor_mul(out=r_sq[:], in0=r_norm[:], in1=r_norm[:])
+        den_m1 = row_numbers("den_m1")
+        nc.vector.scalar_tensor_tensor(
+            out=den_m1[:], in0=r_sq[:], scalar=y_sq[:], in1=r_y2[:], op0=ALU.mult, op1=ALU.add
+        )
+        den = row_numbers("den")
+        nc.vector.tensor_scalar(
+            out=den[:], in0=den_m1[:], scalar1=1.0, scalar2=NORM_MIN, op0=ALU.add, op1=ALU.max
+        )
+        rden = row_numbers("rden")
+        nc.vector.reciprocal(out=rden[:], in_=den[:])
+        sum_sq = row_numbers("sum_sq")
+        nc.vector.scalar_tensor_tensor(
+            out=sum_sq[:], in0=r_sq[:], scalar=y_sq[:], in1=r_y2[:], op0=ALU.add, op1=ALU.add
+        )
+        r2_sq = row_numbers("r2_sq")
+        nc.vector.tensor_mul(out=r2_sq[:], in0=sum_sq[:], in1=rden[:])
+        r2_sq_clip = row_numbers("r2_sq_clip")
+        nc.vector.tensor_scalar_max(out=r2_sq_clip[:], in0=r2_sq[:], scalar1=NORM_MIN_SQ)
+        r2_norm = row_numbers("r2_norm")
+        nc.gpsimd.tensor_tensor(out=r2_norm[:], in0=r2_sq_clip[:], in1=half[:], op=ALU.pow)
+        direction(1)
+        direction(2)
+        r2_clip = row_numbers("r2_clip")
+        nc.vector.tensor_scalar_min(out=r2_clip[:], in0=r2_norm[:], scalar1=BOUND)
+        ln_up2 = row_numbers("ln_up2")
+        nc.scalar.activation(out=ln_up2[:], in_=r2_clip[:], func=ACT.Ln, bias=1.0, scale=1.0)
+        ln_dn2 = row_numbers("ln_dn2")
+        nc.scalar.activation(out=ln_dn2[:], in_=r2_clip[:], func=ACT.Ln, bias=1.0, scale=-1.0)
+        load_table(ACT.Tanh, "warm_tanh_b")
+        r2_rnorm = row_numbers("r2_rnorm")
+        nc.vector.reciprocal(out=r2_rnorm[:], in_=r2_norm[:])
+        z_coef = row_numbers("z_coef")
+        nc.vector.tensor_mul(out=z_coef[:], in0=xt_coef[:], in1=rden[:])
+        z_unit = row_numbers("z_unit")
+        nc.vector.tensor_mul(out=z_unit[:], in0=z_coef[:], in1=r2_rnorm[:])
+        direction(3)
+        relu_square_sum(0)
+        artanh2 = row_numbers("artanh2")
+        nc.vector.tensor_sub(out=artanh2[:], in0=ln_up2[:], in1=ln_dn2[:])
+        log_coef = row_numbers("log_coef")
+        nc.vector.scalar_tensor_tensor(
+            out=log_coef[:], in0=artanh2[:], scalar=0.5, in1=z_unit[:],
+            op0=ALU.mult, op1=ALU.mult,
+        )
+        relu_square_sum(1)
+        relu_square_sum(2)
+        relu_square_sum(3)
+
+        relu_norm = row_numbers("relu_norm")
+        nc.gpsimd.tensor_tensor(out=relu_norm[:], in0=relu_sq[:], in1=half[:], op=ALU.pow)
+        v_norm = row_numbers("v_norm")
+        nc.vector.scalar_tensor_tensor(
+            out=v_norm[:], in0=relu_norm[:], scalar=NORM_MIN, in1=log_coef[:],
+            op0=ALU.max, op1=ALU.mult,
+        )
+        v_tanh = row_numbers("v_tanh")
+        nc.scalar.activation(out=v_tanh[:], in_=v_norm[:], func=ACT.Tanh)
+        relu_norm_clip = row_numbers("relu_norm_clip")
+        nc.vector.tensor_scalar_max(out=relu_norm_clip[:], in0=relu_norm[:], scalar1=NORM_MIN)
+        relu_rnorm = row_numbers("relu_rnorm")
+        nc.vector.reciprocal(out=relu_rnorm[:], in_=relu_norm_clip[:])
+        out_coef = row_numbers("out_coef")
+        nc.vector.tensor_mul(out=out_coef[:], in0=v_tanh[:], in1=relu_rnorm[:])
+
+        result = per_tile([P, D], F32, "result")
+        for i in range(TILES):
+            if i % 2 == 0:
+                nc.scalar.activation(
+                    out=result[i][:], in_=z[i][:], func=ACT.Relu, scale=out_coef[:, i : i + 1]
+                )
+            else:
+                nc.vector.tensor_scalar(
+                    out=result[i][:], in0=z[i][:], scalar1=0.0, scalar2=out_coef[:, i : i + 1],
+                    op0=ALU.max, op1=ALU.mult,
+                )
+            nc.sync.dma_start(out=out[i * P : (i + 1) * P, :], in_=result[i][:])

@@ -17,6 +17,8 @@ PACK = 4
 N_ROWS = 512
 D = 512
 TILES = N_ROWS // P
+GROUPS = 2
+PER_GROUP = TILES // GROUPS
 
 BOUND = 1.0 - 168.0 * 2.0 ** -24
 ARTANH_BOUND = 0.5 * math.log((1.0 + BOUND) / (1.0 - BOUND))
@@ -48,9 +50,28 @@ def tile_hnnlayer_s_kernel(tc, h, weight, bias, gamma, beta, out):
         def one_number(name):
             return keep.tile([P, 1], F32, name=name)
 
-        h_sb = per_tile([P, D], BF16, "h_sb")
+        def tiles_of(g):
+            return range(g * PER_GROUP, (g + 1) * PER_GROUP)
+
+        def cols_of(g):
+            return slice(g * PER_GROUP, (g + 1) * PER_GROUP)
+
+        ALL = slice(0, TILES)
+
+        def power(dst, src, exponent, c):
+            nc.gpsimd.tensor_tensor(out=dst[:, c], in0=src[:, c], in1=exponent[:, c], op=ALU.pow)
+
+        def load_table(func, name):
+            unused = one_number(name)
+            nc.scalar.activation(out=unused[:], in_=ones[:], func=func)
+
+        def square_sum(src, total):
+            squares = scrap.tile([P, D], BF16, name="squares")
+            nc.scalar.activation(out=squares[:], in_=src, func=ACT.Square, accum_out=total)
+
+        h_sb = keep.tile([P, TILES, D], BF16, name="h_sb")
         for i in range(TILES):
-            nc.sync.dma_start(out=h_sb[i][:], in_=h[i * P : (i + 1) * P, :])
+            nc.sync.dma_start(out=h_sb[:, i, :], in_=h[i * P : (i + 1) * P, :])
         gamma_bc = keep.tile([P, D], BF16, name="gamma_bc")
         nc.sync.dma_start(out=gamma_bc[:], in_=gamma.partition_broadcast(P))
         bias_bc = keep.tile([P, D], BF16, name="bias_bc")
@@ -70,342 +91,400 @@ def tile_hnnlayer_s_kernel(tc, h, weight, bias, gamma, beta, out):
         nc.vector.memset(ones[:], 1.0)
         ident = keep.tile([P, P], BF16, name="ident")
         make_identity(nc, ident[:])
-
-        def load_table(func, name):
-            unused = one_number(name)
-            nc.scalar.activation(out=unused[:], in_=ones[:], func=func)
-
-        def square_sum(src, total):
-            squares = scrap.tile([P, D], BF16, name="squares")
-            nc.scalar.activation(out=squares[:], in_=src, func=ACT.Square, accum_out=total)
-
         load_table(ACT.Ln, "warm_ln_a")
 
-        first = row_numbers("first")
+        first = h_sb[:, :, 0]
         d = per_tile([P, D], F32, "d")
         d_sum = row_numbers("d_sum")
         d_sq = row_numbers("d_sq")
-        for i in range(TILES):
-            squares = scrap.tile([P, D], BF16, name="squares")
-            nc.scalar.activation(
-                out=squares[:], in_=h_sb[i][:], func=ACT.Square, scale=-1.0,
-                bias=h_sb[i][:, 0:1], accum_out=d_sq[:, i : i + 1],
-            )
-            nc.vector.tensor_scalar(
-                out=d[i][:], in0=h_sb[i][:], scalar1=h_sb[i][:, 0:1], scalar2=None,
-                op0=ALU.subtract, op1=ALU.add, accum_out=d_sum[:, i : i + 1],
-            )
-            nc.vector.tensor_copy(out=first[:, i : i + 1], in_=h_sb[i][:, 0:1])
-        h_sq_a = row_numbers("h_sq_a")
-        nc.vector.scalar_tensor_tensor(
-            out=h_sq_a[:], in0=first[:], scalar=0.5 * D, in1=d_sum[:], op0=ALU.mult, op1=ALU.add
-        )
-        h_sq_b = row_numbers("h_sq_b")
-        nc.vector.scalar_tensor_tensor(
-            out=h_sq_b[:], in0=h_sq_a[:], scalar=2.0, in1=first[:], op0=ALU.mult, op1=ALU.mult
-        )
-        h_sq = row_numbers("h_sq")
-        nc.vector.tensor_add(out=h_sq[:], in0=h_sq_b[:], in1=d_sq[:])
 
-        centred = per_tile([P, D], F32, "centred")
+        def shifted_sums(g):
+            for i in tiles_of(g):
+                squares = scrap.tile([P, D], BF16, name="squares")
+                nc.scalar.activation(
+                    out=squares[:], in_=h_sb[:, i, :], func=ACT.Square, scale=-1.0,
+                    bias=h_sb[:, i, 0:1], accum_out=d_sq[:, i : i + 1],
+                )
+                nc.vector.tensor_scalar(
+                    out=d[i][:], in0=h_sb[:, i, :], scalar1=h_sb[:, i, 0:1], scalar2=None,
+                    op0=ALU.subtract, op1=ALU.add, accum_out=d_sum[:, i : i + 1],
+                )
+
+        h_sq_a = row_numbers("h_sq_a")
+        h_sq_b = row_numbers("h_sq_b")
+        h_sq = row_numbers("h_sq")
+        h_norm = row_numbers("h_norm")
+        h_clip = row_numbers("h_clip")
         d_mean = row_numbers("d_mean")
 
-        def centre(i):
+        def norm_of_h(c):
             nc.vector.scalar_tensor_tensor(
-                out=centred[i][:], in0=d[i][:], scalar=d_mean[:, i : i + 1],
-                in1=gamma_bc[:], op0=ALU.subtract, op1=ALU.mult,
+                out=h_sq_a[:, c], in0=first[:, c], scalar=0.5 * D, in1=d_sum[:, c],
+                op0=ALU.mult, op1=ALU.add,
+            )
+            nc.vector.scalar_tensor_tensor(
+                out=h_sq_b[:, c], in0=h_sq_a[:, c], scalar=2.0, in1=first[:, c],
+                op0=ALU.mult, op1=ALU.mult,
+            )
+            nc.vector.tensor_add(out=h_sq[:, c], in0=h_sq_b[:, c], in1=d_sq[:, c])
+            power(h_norm, h_sq, half, c)
+            nc.gpsimd.tensor_scalar_min(out=h_clip[:, c], in0=h_norm[:, c], scalar1=BOUND)
+            nc.vector.tensor_scalar_mul(out=d_mean[:, c], in0=d_sum[:, c], scalar1=1.0 / D)
+
+        centred = per_tile([P, D], F32, "centred")
+
+        def centre(g):
+            for i in tiles_of(g):
+                nc.vector.scalar_tensor_tensor(
+                    out=centred[i][:], in0=d[i][:], scalar=d_mean[:, i : i + 1],
+                    in1=gamma_bc[:], op0=ALU.subtract, op1=ALU.mult,
+                )
+
+        d_sum_mean = row_numbers("d_sum_mean")
+        dev_sq = row_numbers("dev_sq")
+        eps_h_sq = row_numbers("eps_h_sq")
+
+        def variance(c):
+            nc.vector.tensor_mul(out=d_sum_mean[:, c], in0=d_sum[:, c], in1=d_mean[:, c])
+            nc.vector.tensor_sub(out=dev_sq[:, c], in0=d_sq[:, c], in1=d_sum_mean[:, c])
+            nc.vector.tensor_scalar(
+                out=eps_h_sq[:, c], in0=h_sq[:, c], scalar1=NORM_MIN_SQ, scalar2=LN_EPS,
+                op0=ALU.max, op1=ALU.mult,
             )
 
-        h_norm = row_numbers("h_norm")
-        nc.gpsimd.tensor_tensor(out=h_norm[:], in0=h_sq[:], in1=half[:], op=ALU.pow)
-        h_clip = row_numbers("h_clip")
-        nc.gpsimd.tensor_scalar_min(out=h_clip[:], in0=h_norm[:], scalar1=BOUND)
-        nc.vector.tensor_scalar_mul(out=d_mean[:], in0=d_sum[:], scalar1=1.0 / D)
-        centre(0)
-        centre(1)
-        d_sum_mean = row_numbers("d_sum_mean")
-        nc.vector.tensor_mul(out=d_sum_mean[:], in0=d_sum[:], in1=d_mean[:])
-        dev_sq = row_numbers("dev_sq")
-        nc.vector.tensor_sub(out=dev_sq[:], in0=d_sq[:], in1=d_sum_mean[:])
-        eps_h_sq = row_numbers("eps_h_sq")
-        nc.vector.tensor_scalar(
-            out=eps_h_sq[:], in0=h_sq[:], scalar1=NORM_MIN_SQ, scalar2=LN_EPS,
-            op0=ALU.max, op1=ALU.mult,
-        )
         ln_up = row_numbers("ln_up")
-        nc.scalar.activation(out=ln_up[:], in_=h_clip[:], func=ACT.Ln, bias=1.0, scale=1.0)
         ln_dn = row_numbers("ln_dn")
-        nc.scalar.activation(out=ln_dn[:], in_=h_clip[:], func=ACT.Ln, bias=1.0, scale=-1.0)
-        centre(2)
+
+        def log_of_h(c):
+            nc.scalar.activation(out=ln_up[:, c], in_=h_clip[:, c], func=ACT.Ln, bias=1.0, scale=1.0)
+            nc.scalar.activation(out=ln_dn[:, c], in_=h_clip[:, c], func=ACT.Ln, bias=1.0, scale=-1.0)
+
         theta2 = row_numbers("theta2")
-        nc.vector.tensor_sub(out=theta2[:], in0=ln_up[:], in1=ln_dn[:])
         theta_sq = row_numbers("theta_sq")
-        nc.vector.scalar_tensor_tensor(
-            out=theta_sq[:], in0=theta2[:], scalar=0.25 / D, in1=theta2[:],
-            op0=ALU.mult, op1=ALU.mult,
-        )
         theta_sq_var = row_numbers("theta_sq_var")
-        nc.vector.tensor_mul(out=theta_sq_var[:], in0=theta_sq[:], in1=dev_sq[:])
         k_arg = row_numbers("k_arg")
-        nc.vector.tensor_add(out=k_arg[:], in0=theta_sq_var[:], in1=eps_h_sq[:])
         k_rsqrt = row_numbers("k_rsqrt")
-        nc.gpsimd.tensor_tensor(out=k_rsqrt[:], in0=k_arg[:], in1=neg_half[:], op=ALU.pow)
-        centre(3)
-
-        bias_sq = one_number("bias_sq")
-        square_sum(bias_bc[:], bias_sq[:])
-        load_table(ACT.Tanh, "warm_tanh_a")
-        bias_sq_clip = one_number("bias_sq_clip")
-        nc.vector.tensor_scalar_max(out=bias_sq_clip[:], in0=bias_sq[:], scalar1=NORM_MIN_SQ)
-        bias_norm = one_number("bias_norm")
-        nc.gpsimd.tensor_tensor(
-            out=bias_norm[:], in0=bias_sq_clip[:], in1=half[:, 0:1], op=ALU.pow
-        )
-
         k = row_numbers("k")
-        nc.vector.scalar_tensor_tensor(
-            out=k[:], in0=theta2[:], scalar=0.5, in1=k_rsqrt[:], op0=ALU.mult, op1=ALU.mult
-        )
+
+        def layer_norm_scale(c):
+            nc.vector.tensor_sub(out=theta2[:, c], in0=ln_up[:, c], in1=ln_dn[:, c])
+            nc.vector.scalar_tensor_tensor(
+                out=theta_sq[:, c], in0=theta2[:, c], scalar=0.25 / D, in1=theta2[:, c],
+                op0=ALU.mult, op1=ALU.mult,
+            )
+            nc.vector.tensor_mul(out=theta_sq_var[:, c], in0=theta_sq[:, c], in1=dev_sq[:, c])
+            nc.vector.tensor_add(out=k_arg[:, c], in0=theta_sq_var[:, c], in1=eps_h_sq[:, c])
+            power(k_rsqrt, k_arg, neg_half, c)
 
         x = per_tile([P, D], F32, "x")
         x_sq = row_numbers("x_sq")
-        for i in range(TILES):
-            nc.vector.scalar_tensor_tensor(
-                out=x[i][:], in0=centred[i][:], scalar=k[:, i : i + 1], in1=beta_bc[:],
-                op0=ALU.mult, op1=ALU.add,
-            )
-            square_sum(x[i][:], x_sq[:, i : i + 1])
         x_rnorm = row_numbers("x_rnorm")
-        nc.gpsimd.tensor_tensor(out=x_rnorm[:], in0=x_sq[:], in1=neg_half[:], op=ALU.pow)
+
+        def layer_norm(g):
+            c = cols_of(g)
+            nc.vector.scalar_tensor_tensor(
+                out=k[:, c], in0=theta2[:, c], scalar=0.5, in1=k_rsqrt[:, c],
+                op0=ALU.mult, op1=ALU.mult,
+            )
+            for i in tiles_of(g):
+                nc.vector.scalar_tensor_tensor(
+                    out=x[i][:], in0=centred[i][:], scalar=k[:, i : i + 1], in1=beta_bc[:],
+                    op0=ALU.mult, op1=ALU.add,
+                )
+                square_sum(x[i][:], x_sq[:, i : i + 1])
+            power(x_rnorm, x_sq, neg_half, c)
+
+        bias_sq = one_number("bias_sq")
+        bias_sq_clip = one_number("bias_sq_clip")
+        bias_norm = one_number("bias_norm")
+        bias_tanh = one_number("bias_tanh")
+        bias_rnorm = one_number("bias_rnorm")
+        y_scale = one_number("y_scale")
+        neg_y_scale = one_number("neg_y_scale")
+        y_sq = one_number("y_sq")
+        one_plus_y_sq = one_number("one_plus_y_sq")
+
+        def bias_square_sum():
+            square_sum(bias_bc[:], bias_sq[:])
+            load_table(ACT.Tanh, "warm_tanh_a")
+
+        def bias_norm_steps():
+            nc.vector.tensor_scalar_max(out=bias_sq_clip[:], in0=bias_sq[:], scalar1=NORM_MIN_SQ)
+            nc.gpsimd.tensor_tensor(
+                out=bias_norm[:], in0=bias_sq_clip[:], in1=half[:, 0:1], op=ALU.pow
+            )
+
+        def bias_point_steps():
+            nc.scalar.activation(out=bias_tanh[:], in_=bias_norm[:], func=ACT.Tanh)
+            nc.vector.reciprocal(out=bias_rnorm[:], in_=bias_norm[:])
+            nc.vector.tensor_mul(out=y_scale[:], in0=bias_tanh[:], in1=bias_rnorm[:])
+            nc.vector.tensor_scalar_mul(out=neg_y_scale[:], in0=y_scale[:], scalar1=-1.0)
+            nc.vector.tensor_scalar(
+                out=y_sq[:], in0=bias_sq[:], scalar1=y_scale[:], scalar2=y_scale[:],
+                op0=ALU.mult, op1=ALU.mult,
+            )
+            nc.vector.tensor_scalar_add(out=one_plus_y_sq[:], in0=y_sq[:], scalar1=1.0)
 
         w_grouped = keep.tile([P, D, PACK], BF16, name="w_grouped", align_bytes=64)
         w_codes = keep.tile([P, D], U32, name="w_codes", align_bytes=64)
         w_scales = keep.tile([P, D], U8, name="w_scales", align_bytes=64)
-        w_t = []
-        for pair in range(2):
-            w_t.append(psum_tr.tile([P, 2, PACK, P], BF16, name="w_t%d" % pair, tag="tr"))
-            for a in range(2):
-                for t in range(PACK):
-                    nc.tensor.transpose(
-                        out=w_t[pair][:, a, t, :],
-                        in_=w_sb[:, 2 * pair + a, t * P : (t + 1) * P],
-                        identity=ident[:],
-                    )
-        bias_tanh = one_number("bias_tanh")
-        nc.scalar.activation(out=bias_tanh[:], in_=bias_norm[:], func=ACT.Tanh)
-        nc.scalar.copy(
-            out=w_grouped[:, 0 : 2 * P, :].rearrange("p (a r) t -> p a r t", a=2),
-            in_=w_t[0][:].rearrange("p a t r -> p a r t"),
-        )
-        nc.vector.tensor_copy(
-            out=w_grouped[:, 2 * P : 4 * P, :].rearrange("p (a r) t -> p a r t", a=2),
-            in_=w_t[1][:].rearrange("p a t r -> p a r t"),
-        )
+        w_t = [psum_tr.tile([P, 2, PACK, P], BF16, name="w_t%d" % b, tag="tr") for b in range(2)]
 
-        bias_rnorm = one_number("bias_rnorm")
-        nc.vector.reciprocal(out=bias_rnorm[:], in_=bias_norm[:])
-        y_scale = one_number("y_scale")
-        nc.vector.tensor_mul(out=y_scale[:], in0=bias_tanh[:], in1=bias_rnorm[:])
-        neg_y_scale = one_number("neg_y_scale")
-        nc.vector.tensor_scalar_mul(out=neg_y_scale[:], in0=y_scale[:], scalar1=-1.0)
-        y_sq = one_number("y_sq")
-        nc.vector.tensor_scalar(
-            out=y_sq[:], in0=bias_sq[:], scalar1=y_scale[:], scalar2=y_scale[:],
-            op0=ALU.mult, op1=ALU.mult,
-        )
-        one_plus_y_sq = one_number("one_plus_y_sq")
-        nc.vector.tensor_scalar_add(out=one_plus_y_sq[:], in0=y_sq[:], scalar1=1.0)
+        def transpose_weight():
+            for b in range(2):
+                for a in range(2):
+                    for t in range(PACK):
+                        nc.tensor.transpose(
+                            out=w_t[b][:, a, t, :],
+                            in_=w_sb[:, 2 * b + a, t * P : (t + 1) * P],
+                            identity=ident[:],
+                        )
+
+        def regroup_weight(b):
+            nc.scalar.copy(
+                out=w_grouped[:, 2 * b * P : 2 * (b + 1) * P, :].rearrange(
+                    "p (a r) t -> p a r t", a=2
+                ),
+                in_=w_t[b][:].rearrange("p a t r -> p a r t"),
+            )
+
+        def quantise_weight():
+            nc.vector.quantize_mx(
+                out=w_codes[:].bitcast(FP8X4),
+                scales=w_scales[:],
+                in_=w_grouped[:].rearrange("p c t -> p (c t)"),
+            )
 
         shrink = row_numbers("shrink")
-        nc.vector.tensor_scalar(
-            out=shrink[:], in0=x_rnorm[:], scalar1=ARTANH_BOUND, scalar2=1.0,
-            op0=ALU.mult, op1=ALU.min,
-        )
-        nc.vector.quantize_mx(
-            out=w_codes[:].bitcast(FP8X4),
-            scales=w_scales[:],
-            in_=w_grouped[:].rearrange("p c t -> p (c t)"),
-        )
-
         u = per_tile([P, D], BF16, "u")
+        u_t = {}
         u_grouped = per_tile([P, P, PACK], BF16, "u_grouped")
         u_codes = per_tile([P, P], U32, "u_codes")
         u_scales = per_tile([P, P], U8, "u_scales")
         xt = [psum_xt.tile([P, D], F32, name="xt%d" % i) for i in range(TILES)]
         xt_sq = row_numbers("xt_sq")
         xt_y = row_numbers("xt_y")
-
-        def make_u(i):
-            nc.scalar.activation(
-                out=u[i][:], in_=x[i][:], func=ACT.Copy, scale=shrink[:, i : i + 1]
-            )
-            u_t = psum_tr.tile([P, PACK, P], BF16, name="u_t", tag="tr")
-            for t in range(PACK):
-                nc.tensor.transpose(
-                    out=u_t[:, t, :], in_=u[i][:, t * P : (t + 1) * P], identity=ident[:]
-                )
-            nc.vector.tensor_copy(out=u_grouped[i][:], in_=u_t[:].rearrange("p t r -> p r t"))
-
-        def multiply(i):
-            nc.vector.quantize_mx(
-                out=u_codes[i][:].bitcast(FP8X4),
-                scales=u_scales[i][:],
-                in_=u_grouped[i][:].rearrange("p r t -> p (r t)"),
-            )
-            nc.tensor.matmul_mx(
-                out=xt[i][:],
-                lhsT=u_codes[i][:].bitcast(FP8X4),
-                lhsT_scale=u_scales[i][:],
-                rhs=w_codes[:].bitcast(FP8X4),
-                rhs_scale=w_scales[:],
-                start=True,
-                stop=True,
-            )
-
-        def row_sums(i):
-            square_sum(xt[i][:], xt_sq[:, i : i + 1])
-            products = scrap.tile([P, D], F32, name="products")
-            nc.vector.scalar_tensor_tensor(
-                out=products[:], in0=xt[i][:], scalar=y_scale[:], in1=bias_bc[:],
-                op0=ALU.mult, op1=ALU.mult, accum_out=xt_y[:, i : i + 1],
-            )
-
-        for step in range(TILES + 2):
-            if step < TILES:
-                make_u(step)
-            if 1 <= step <= TILES:
-                multiply(step - 1)
-            if step >= 2:
-                row_sums(step - 2)
-
         xt_norm = row_numbers("xt_norm")
-        nc.gpsimd.tensor_tensor(out=xt_norm[:], in0=xt_sq[:], in1=half[:], op=ALU.pow)
+
+        def make_u(g):
+            c = cols_of(g)
+            nc.vector.tensor_scalar(
+                out=shrink[:, c], in0=x_rnorm[:, c], scalar1=ARTANH_BOUND, scalar2=1.0,
+                op0=ALU.mult, op1=ALU.min,
+            )
+            for i in tiles_of(g):
+                nc.vector.tensor_scalar_mul(out=u[i][:], in0=x[i][:], scalar1=shrink[:, i : i + 1])
+                u_t[i] = psum_tr.tile([P, PACK, P], BF16, name="u_t", tag="tr")
+                for t in range(PACK):
+                    nc.tensor.transpose(
+                        out=u_t[i][:, t, :], in_=u[i][:, t * P : (t + 1) * P], identity=ident[:]
+                    )
+
+        def regroup_u(g):
+            for i in tiles_of(g):
+                nc.scalar.copy(out=u_grouped[i][:], in_=u_t[i][:].rearrange("p t r -> p r t"))
+
+        def multiply(g):
+            for i in tiles_of(g):
+                nc.vector.quantize_mx(
+                    out=u_codes[i][:].bitcast(FP8X4),
+                    scales=u_scales[i][:],
+                    in_=u_grouped[i][:].rearrange("p r t -> p (r t)"),
+                )
+                nc.tensor.matmul_mx(
+                    out=xt[i][:],
+                    lhsT=u_codes[i][:].bitcast(FP8X4),
+                    lhsT_scale=u_scales[i][:],
+                    rhs=w_codes[:].bitcast(FP8X4),
+                    rhs_scale=w_scales[:],
+                    start=True,
+                    stop=True,
+                )
+
+        def row_sums(g):
+            for i in tiles_of(g):
+                square_sum(xt[i][:], xt_sq[:, i : i + 1])
+                products = scrap.tile([P, D], F32, name="products")
+                nc.vector.scalar_tensor_tensor(
+                    out=products[:], in0=xt[i][:], scalar=y_scale[:], in1=bias_bc[:],
+                    op0=ALU.mult, op1=ALU.mult, accum_out=xt_y[:, i : i + 1],
+                )
+            power(xt_norm, xt_sq, half, cols_of(g))
+
         r_norm = row_numbers("r_norm")
-        nc.scalar.activation(out=r_norm[:], in_=xt_norm[:], func=ACT.Tanh)
-        load_table(ACT.Ln, "warm_ln_b")
         xt_norm_clip = row_numbers("xt_norm_clip")
-        nc.vector.tensor_scalar_max(out=xt_norm_clip[:], in0=xt_norm[:], scalar1=NORM_MIN)
         xt_rnorm = row_numbers("xt_rnorm")
-        nc.vector.reciprocal(out=xt_rnorm[:], in_=xt_norm_clip[:])
         xt_y_unit2 = row_numbers("xt_y_unit2")
-        nc.vector.scalar_tensor_tensor(
-            out=xt_y_unit2[:], in0=xt_rnorm[:], scalar=2.0, in1=xt_y[:],
-            op0=ALU.mult, op1=ALU.mult,
-        )
+
+        def exp_map(c):
+            nc.scalar.activation(out=r_norm[:, c], in_=xt_norm[:, c], func=ACT.Tanh)
+            nc.vector.tensor_scalar_max(out=xt_norm_clip[:, c], in0=xt_norm[:, c], scalar1=NORM_MIN)
+            nc.vector.reciprocal(out=xt_rnorm[:, c], in_=xt_norm_clip[:, c])
+            nc.vector.scalar_tensor_tensor(
+                out=xt_y_unit2[:, c], in0=xt_rnorm[:, c], scalar=2.0, in1=xt_y[:, c],
+                op0=ALU.mult, op1=ALU.mult,
+            )
+
         r_y2 = row_numbers("r_y2")
-        nc.vector.tensor_mul(out=r_y2[:], in0=r_norm[:], in1=xt_y_unit2[:])
         rho = row_numbers("rho")
-        nc.vector.tensor_mul(out=rho[:], in0=r_norm[:], in1=xt_rnorm[:])
         neg_ys_r_sq = row_numbers("neg_ys_r_sq")
-        nc.vector.scalar_tensor_tensor(
-            out=neg_ys_r_sq[:], in0=r_norm[:], scalar=neg_y_scale[:], in1=r_norm[:],
-            op0=ALU.mult, op1=ALU.mult,
-        )
         xt_coef = row_numbers("xt_coef")
-        nc.vector.scalar_tensor_tensor(
-            out=xt_coef[:], in0=r_y2[:], scalar=one_plus_y_sq[:], in1=rho[:],
-            op0=ALU.add, op1=ALU.mult,
-        )
         xt_rcoef = row_numbers("xt_rcoef")
-        nc.vector.reciprocal(out=xt_rcoef[:], in_=xt_coef[:])
         bias_coef = row_numbers("bias_coef")
-        nc.vector.scalar_tensor_tensor(
-            out=bias_coef[:], in0=neg_ys_r_sq[:], scalar=y_scale[:], in1=xt_rcoef[:],
-            op0=ALU.add, op1=ALU.mult,
-        )
+
+        def moebius_coefficients(c):
+            nc.vector.tensor_mul(out=r_y2[:, c], in0=r_norm[:, c], in1=xt_y_unit2[:, c])
+            nc.vector.tensor_mul(out=rho[:, c], in0=r_norm[:, c], in1=xt_rnorm[:, c])
+            nc.vector.scalar_tensor_tensor(
+                out=neg_ys_r_sq[:, c], in0=r_norm[:, c], scalar=neg_y_scale[:], in1=r_norm[:, c],
+                op0=ALU.mult, op1=ALU.mult,
+            )
+            nc.vector.scalar_tensor_tensor(
+                out=xt_coef[:, c], in0=r_y2[:, c], scalar=one_plus_y_sq[:], in1=rho[:, c],
+                op0=ALU.add, op1=ALU.mult,
+            )
+            nc.vector.reciprocal(out=xt_rcoef[:, c], in_=xt_coef[:, c])
+            nc.vector.scalar_tensor_tensor(
+                out=bias_coef[:, c], in0=neg_ys_r_sq[:, c], scalar=y_scale[:], in1=xt_rcoef[:, c],
+                op0=ALU.add, op1=ALU.mult,
+            )
 
         z = per_tile([P, D], F32, "z")
         relu_sq = row_numbers("relu_sq")
+        relu_norm = row_numbers("relu_norm")
 
-        def direction(i):
+        def direction(g):
+            for i in tiles_of(g):
+                nc.vector.scalar_tensor_tensor(
+                    out=z[i][:], in0=bias_bc[:], scalar=bias_coef[:, i : i + 1], in1=xt[i][:],
+                    op0=ALU.mult, op1=ALU.add,
+                )
+
+        def relu_square_sums(g):
+            for i in tiles_of(g):
+                products = scrap.tile([P, D], F32, name="products")
+                nc.vector.scalar_tensor_tensor(
+                    out=products[:], in0=z[i][:], scalar=0.0, in1=z[i][:],
+                    op0=ALU.max, op1=ALU.mult, accum_out=relu_sq[:, i : i + 1],
+                )
+            power(relu_norm, relu_sq, half, cols_of(g))
+
+        r_sq = row_numbers("r_sq")
+        den_m1 = row_numbers("den_m1")
+        den = row_numbers("den")
+        sum_sq = row_numbers("sum_sq")
+        sum_den = row_numbers("sum_den")
+        sum_den_clip = row_numbers("sum_den_clip")
+        sum_den_rsqrt = row_numbers("sum_den_rsqrt")
+        r2_norm = row_numbers("r2_norm")
+        r2_clip = row_numbers("r2_clip")
+
+        def norm_of_r2(c):
+            nc.vector.tensor_mul(out=r_sq[:, c], in0=r_norm[:, c], in1=r_norm[:, c])
             nc.vector.scalar_tensor_tensor(
-                out=z[i][:], in0=bias_bc[:], scalar=bias_coef[:, i : i + 1], in1=xt[i][:],
+                out=den_m1[:, c], in0=r_sq[:, c], scalar=y_sq[:], in1=r_y2[:, c],
                 op0=ALU.mult, op1=ALU.add,
             )
-
-        def relu_square_sum(i):
-            products = scrap.tile([P, D], F32, name="products")
+            nc.vector.tensor_scalar(
+                out=den[:, c], in0=den_m1[:, c], scalar1=1.0, scalar2=NORM_MIN,
+                op0=ALU.add, op1=ALU.max,
+            )
             nc.vector.scalar_tensor_tensor(
-                out=products[:], in0=z[i][:], scalar=0.0, in1=z[i][:],
-                op0=ALU.max, op1=ALU.mult, accum_out=relu_sq[:, i : i + 1],
+                out=sum_sq[:, c], in0=r_sq[:, c], scalar=y_sq[:], in1=r_y2[:, c],
+                op0=ALU.add, op1=ALU.add,
+            )
+            nc.vector.tensor_mul(out=sum_den[:, c], in0=sum_sq[:, c], in1=den[:, c])
+            nc.vector.tensor_scalar_max(out=sum_den_clip[:, c], in0=sum_den[:, c], scalar1=NORM_MIN_SQ)
+            power(sum_den_rsqrt, sum_den_clip, neg_half, c)
+            nc.gpsimd.tensor_tensor(
+                out=r2_norm[:, c], in0=sum_sq[:, c], in1=sum_den_rsqrt[:, c], op=ALU.mult
+            )
+            nc.gpsimd.tensor_scalar_min(out=r2_clip[:, c], in0=r2_norm[:, c], scalar1=BOUND)
+
+        ln_up2 = row_numbers("ln_up2")
+        ln_dn2 = row_numbers("ln_dn2")
+        z_unit = row_numbers("z_unit")
+        artanh2 = row_numbers("artanh2")
+        log_coef = row_numbers("log_coef")
+
+        def log_of_r2(c):
+            nc.scalar.activation(out=ln_up2[:, c], in_=r2_clip[:, c], func=ACT.Ln, bias=1.0, scale=1.0)
+            nc.scalar.activation(out=ln_dn2[:, c], in_=r2_clip[:, c], func=ACT.Ln, bias=1.0, scale=-1.0)
+
+        def log_map_coefficient(c):
+            nc.vector.tensor_mul(out=z_unit[:, c], in0=xt_coef[:, c], in1=sum_den_rsqrt[:, c])
+            nc.vector.tensor_sub(out=artanh2[:, c], in0=ln_up2[:, c], in1=ln_dn2[:, c])
+            nc.vector.scalar_tensor_tensor(
+                out=log_coef[:, c], in0=artanh2[:, c], scalar=0.5, in1=z_unit[:, c],
+                op0=ALU.mult, op1=ALU.mult,
             )
 
-        direction(0)
-        r_sq = row_numbers("r_sq")
-        nc.vector.tensor_mul(out=r_sq[:], in0=r_norm[:], in1=r_norm[:])
-        den_m1 = row_numbers("den_m1")
-        nc.vector.scalar_tensor_tensor(
-            out=den_m1[:], in0=r_sq[:], scalar=y_sq[:], in1=r_y2[:], op0=ALU.mult, op1=ALU.add
-        )
-        den = row_numbers("den")
-        nc.vector.tensor_scalar(
-            out=den[:], in0=den_m1[:], scalar1=1.0, scalar2=NORM_MIN, op0=ALU.add, op1=ALU.max
-        )
-        rden = row_numbers("rden")
-        nc.vector.reciprocal(out=rden[:], in_=den[:])
-        sum_sq = row_numbers("sum_sq")
-        nc.vector.scalar_tensor_tensor(
-            out=sum_sq[:], in0=r_sq[:], scalar=y_sq[:], in1=r_y2[:], op0=ALU.add, op1=ALU.add
-        )
-        r2_sq = row_numbers("r2_sq")
-        nc.vector.tensor_mul(out=r2_sq[:], in0=sum_sq[:], in1=rden[:])
-        r2_sq_clip = row_numbers("r2_sq_clip")
-        nc.vector.tensor_scalar_max(out=r2_sq_clip[:], in0=r2_sq[:], scalar1=NORM_MIN_SQ)
-        r2_norm = row_numbers("r2_norm")
-        nc.gpsimd.tensor_tensor(out=r2_norm[:], in0=r2_sq_clip[:], in1=half[:], op=ALU.pow)
-        direction(1)
-        direction(2)
-        r2_clip = row_numbers("r2_clip")
-        nc.vector.tensor_scalar_min(out=r2_clip[:], in0=r2_norm[:], scalar1=BOUND)
-        ln_up2 = row_numbers("ln_up2")
-        nc.scalar.activation(out=ln_up2[:], in_=r2_clip[:], func=ACT.Ln, bias=1.0, scale=1.0)
-        ln_dn2 = row_numbers("ln_dn2")
-        nc.scalar.activation(out=ln_dn2[:], in_=r2_clip[:], func=ACT.Ln, bias=1.0, scale=-1.0)
-        load_table(ACT.Tanh, "warm_tanh_b")
-        r2_rnorm = row_numbers("r2_rnorm")
-        nc.vector.reciprocal(out=r2_rnorm[:], in_=r2_norm[:])
-        z_coef = row_numbers("z_coef")
-        nc.vector.tensor_mul(out=z_coef[:], in0=xt_coef[:], in1=rden[:])
-        z_unit = row_numbers("z_unit")
-        nc.vector.tensor_mul(out=z_unit[:], in0=z_coef[:], in1=r2_rnorm[:])
-        direction(3)
-        relu_square_sum(0)
-        artanh2 = row_numbers("artanh2")
-        nc.vector.tensor_sub(out=artanh2[:], in0=ln_up2[:], in1=ln_dn2[:])
-        log_coef = row_numbers("log_coef")
-        nc.vector.scalar_tensor_tensor(
-            out=log_coef[:], in0=artanh2[:], scalar=0.5, in1=z_unit[:],
-            op0=ALU.mult, op1=ALU.mult,
-        )
-        relu_square_sum(1)
-        relu_square_sum(2)
-        relu_square_sum(3)
-
-        relu_norm = row_numbers("relu_norm")
-        nc.gpsimd.tensor_tensor(out=relu_norm[:], in0=relu_sq[:], in1=half[:], op=ALU.pow)
         v_norm = row_numbers("v_norm")
-        nc.vector.scalar_tensor_tensor(
-            out=v_norm[:], in0=relu_norm[:], scalar=NORM_MIN, in1=log_coef[:],
-            op0=ALU.max, op1=ALU.mult,
-        )
         v_tanh = row_numbers("v_tanh")
-        nc.scalar.activation(out=v_tanh[:], in_=v_norm[:], func=ACT.Tanh)
         relu_norm_clip = row_numbers("relu_norm_clip")
-        nc.vector.tensor_scalar_max(out=relu_norm_clip[:], in0=relu_norm[:], scalar1=NORM_MIN)
         relu_rnorm = row_numbers("relu_rnorm")
-        nc.vector.reciprocal(out=relu_rnorm[:], in_=relu_norm_clip[:])
         out_coef = row_numbers("out_coef")
-        nc.vector.tensor_mul(out=out_coef[:], in0=v_tanh[:], in1=relu_rnorm[:])
-
         result = per_tile([P, D], F32, "result")
-        for i in range(TILES):
-            if i % 2 == 0:
-                nc.scalar.activation(
-                    out=result[i][:], in_=z[i][:], func=ACT.Relu, scale=out_coef[:, i : i + 1]
-                )
-            else:
-                nc.vector.tensor_scalar(
-                    out=result[i][:], in0=z[i][:], scalar1=0.0, scalar2=out_coef[:, i : i + 1],
-                    op0=ALU.max, op1=ALU.mult,
-                )
-            nc.sync.dma_start(out=out[i * P : (i + 1) * P, :], in_=result[i][:])
+
+        def out_coefficient(c):
+            nc.vector.scalar_tensor_tensor(
+                out=v_norm[:, c], in0=relu_norm[:, c], scalar=NORM_MIN, in1=log_coef[:, c],
+                op0=ALU.max, op1=ALU.mult,
+            )
+            nc.scalar.activation(out=v_tanh[:, c], in_=v_norm[:, c], func=ACT.Tanh)
+            nc.vector.tensor_scalar_max(out=relu_norm_clip[:, c], in0=relu_norm[:, c], scalar1=NORM_MIN)
+            nc.vector.reciprocal(out=relu_rnorm[:, c], in_=relu_norm_clip[:, c])
+            nc.vector.tensor_mul(out=out_coef[:, c], in0=v_tanh[:, c], in1=relu_rnorm[:, c])
+
+        def finish(g):
+            for i in tiles_of(g):
+                if i % 2 == 0:
+                    nc.scalar.activation(
+                        out=result[i][:], in_=z[i][:], func=ACT.Relu, scale=out_coef[:, i : i + 1]
+                    )
+                else:
+                    nc.vector.tensor_scalar(
+                        out=result[i][:], in0=z[i][:], scalar1=0.0, scalar2=out_coef[:, i : i + 1],
+                        op0=ALU.max, op1=ALU.mult,
+                    )
+                nc.sync.dma_start(out=out[i * P : (i + 1) * P, :], in_=result[i][:])
+
+        transpose_weight()
+        shifted_sums(0)
+        shifted_sums(1)
+        norm_of_h(ALL)
+        centre(0)
+        log_of_h(ALL)
+        variance(ALL)
+        centre(1)
+        bias_square_sum()
+        layer_norm_scale(ALL)
+        bias_norm_steps()
+        regroup_weight(0)
+        regroup_weight(1)
+        layer_norm(0)
+        layer_norm(1)
+        quantise_weight()
+        make_u(0)
+        bias_point_steps()
+        regroup_u(0)
+        make_u(1)
+        multiply(0)
+        regroup_u(1)
+        row_sums(0)
+        multiply(1)
+        row_sums(1)
+        exp_map(ALL)
+        moebius_coefficients(ALL)
+        load_table(ACT.Ln, "warm_ln_b")
+        norm_of_r2(ALL)
+        direction(0)
+        direction(1)
+        log_of_r2(ALL)
+        load_table(ACT.Tanh, "warm_tanh_b")
+        relu_square_sums(0)
+        log_map_coefficient(ALL)
+        relu_square_sums(1)
+        out_coefficient(ALL)
+        finish(0)
+        finish(1)

@@ -17,14 +17,13 @@ PACK = 4
 N_ROWS = 512
 D = 512
 TILES = N_ROWS // P
-GROUPS = 2
-PER_GROUP = TILES // GROUPS
 
 BOUND = 1.0 - 168.0 * 2.0 ** -24
 ARTANH_BOUND = 0.5 * math.log((1.0 + BOUND) / (1.0 - BOUND))
 LN_EPS = 1e-5
 NORM_MIN = 1e-15
 NORM_MIN_SQ = 1e-30
+SUM_SQ_MIN = 1e-20
 
 FLOPS = 2 * N_ROWS * D * D
 
@@ -50,15 +49,11 @@ def tile_hnnlayer_s_kernel(tc, h, weight, bias, gamma, beta, out):
         def one_number(name):
             return keep.tile([P, 1], F32, name=name)
 
-        def tiles_of(g):
-            return range(g * PER_GROUP, (g + 1) * PER_GROUP)
+        def cols(rows):
+            return slice(rows[0], rows[-1] + 1)
 
-        def cols_of(g):
-            return slice(g * PER_GROUP, (g + 1) * PER_GROUP)
-
-        ALL = slice(0, TILES)
-
-        def power(dst, src, exponent, c):
+        def power(dst, src, exponent, rows):
+            c = cols(rows)
             nc.gpsimd.tensor_tensor(out=dst[:, c], in0=src[:, c], in1=exponent[:, c], op=ALU.pow)
 
         def load_table(func, name):
@@ -98,8 +93,8 @@ def tile_hnnlayer_s_kernel(tc, h, weight, bias, gamma, beta, out):
         d_sum = row_numbers("d_sum")
         d_sq = row_numbers("d_sq")
 
-        def shifted_sums(g):
-            for i in tiles_of(g):
+        def shifted_sums(rows):
+            for i in rows:
                 squares = scrap.tile([P, D], BF16, name="squares")
                 nc.scalar.activation(
                     out=squares[:], in_=h_sb[:, i, :], func=ACT.Square, scale=-1.0,
@@ -110,6 +105,8 @@ def tile_hnnlayer_s_kernel(tc, h, weight, bias, gamma, beta, out):
                     op0=ALU.subtract, op1=ALU.add, accum_out=d_sum[:, i : i + 1],
                 )
 
+        first_x2 = row_numbers("first_x2")
+        first_sq = row_numbers("first_sq")
         h_sq_a = row_numbers("h_sq_a")
         h_sq_b = row_numbers("h_sq_b")
         h_sq = row_numbers("h_sq")
@@ -117,24 +114,27 @@ def tile_hnnlayer_s_kernel(tc, h, weight, bias, gamma, beta, out):
         h_clip = row_numbers("h_clip")
         d_mean = row_numbers("d_mean")
 
-        def norm_of_h(c):
+        def first_terms(rows):
+            c = cols(rows)
+            nc.vector.tensor_scalar_mul(out=first_x2[:, c], in0=first[:, c], scalar1=2.0)
             nc.vector.scalar_tensor_tensor(
-                out=h_sq_a[:, c], in0=first[:, c], scalar=0.5 * D, in1=d_sum[:, c],
-                op0=ALU.mult, op1=ALU.add,
-            )
-            nc.vector.scalar_tensor_tensor(
-                out=h_sq_b[:, c], in0=h_sq_a[:, c], scalar=2.0, in1=first[:, c],
+                out=first_sq[:, c], in0=first[:, c], scalar=1.0 * D, in1=first[:, c],
                 op0=ALU.mult, op1=ALU.mult,
             )
-            nc.vector.tensor_add(out=h_sq[:, c], in0=h_sq_b[:, c], in1=d_sq[:, c])
-            power(h_norm, h_sq, half, c)
+
+        def norm_of_h(rows):
+            c = cols(rows)
+            nc.vector.tensor_add(out=h_sq_a[:, c], in0=d_sq[:, c], in1=first_sq[:, c])
+            nc.vector.tensor_mul(out=h_sq_b[:, c], in0=d_sum[:, c], in1=first_x2[:, c])
+            nc.vector.tensor_add(out=h_sq[:, c], in0=h_sq_a[:, c], in1=h_sq_b[:, c])
+            power(h_norm, h_sq, half, rows)
             nc.gpsimd.tensor_scalar_min(out=h_clip[:, c], in0=h_norm[:, c], scalar1=BOUND)
             nc.vector.tensor_scalar_mul(out=d_mean[:, c], in0=d_sum[:, c], scalar1=1.0 / D)
 
         centred = per_tile([P, D], F32, "centred")
 
-        def centre(g):
-            for i in tiles_of(g):
+        def centre(rows):
+            for i in rows:
                 nc.vector.scalar_tensor_tensor(
                     out=centred[i][:], in0=d[i][:], scalar=d_mean[:, i : i + 1],
                     in1=gamma_bc[:], op0=ALU.subtract, op1=ALU.mult,
@@ -144,7 +144,8 @@ def tile_hnnlayer_s_kernel(tc, h, weight, bias, gamma, beta, out):
         dev_sq = row_numbers("dev_sq")
         eps_h_sq = row_numbers("eps_h_sq")
 
-        def variance(c):
+        def variance(rows):
+            c = cols(rows)
             nc.vector.tensor_mul(out=d_sum_mean[:, c], in0=d_sum[:, c], in1=d_mean[:, c])
             nc.vector.tensor_sub(out=dev_sq[:, c], in0=d_sq[:, c], in1=d_sum_mean[:, c])
             nc.vector.tensor_scalar(
@@ -155,7 +156,8 @@ def tile_hnnlayer_s_kernel(tc, h, weight, bias, gamma, beta, out):
         ln_up = row_numbers("ln_up")
         ln_dn = row_numbers("ln_dn")
 
-        def log_of_h(c):
+        def log_of_h(rows):
+            c = cols(rows)
             nc.scalar.activation(out=ln_up[:, c], in_=h_clip[:, c], func=ACT.Ln, bias=1.0, scale=1.0)
             nc.scalar.activation(out=ln_dn[:, c], in_=h_clip[:, c], func=ACT.Ln, bias=1.0, scale=-1.0)
 
@@ -166,7 +168,8 @@ def tile_hnnlayer_s_kernel(tc, h, weight, bias, gamma, beta, out):
         k_rsqrt = row_numbers("k_rsqrt")
         k = row_numbers("k")
 
-        def layer_norm_scale(c):
+        def layer_norm_scale(rows):
+            c = cols(rows)
             nc.vector.tensor_sub(out=theta2[:, c], in0=ln_up[:, c], in1=ln_dn[:, c])
             nc.vector.scalar_tensor_tensor(
                 out=theta_sq[:, c], in0=theta2[:, c], scalar=0.25 / D, in1=theta2[:, c],
@@ -174,25 +177,26 @@ def tile_hnnlayer_s_kernel(tc, h, weight, bias, gamma, beta, out):
             )
             nc.vector.tensor_mul(out=theta_sq_var[:, c], in0=theta_sq[:, c], in1=dev_sq[:, c])
             nc.vector.tensor_add(out=k_arg[:, c], in0=theta_sq_var[:, c], in1=eps_h_sq[:, c])
-            power(k_rsqrt, k_arg, neg_half, c)
+            power(k_rsqrt, k_arg, neg_half, rows)
 
         x = per_tile([P, D], F32, "x")
         x_sq = row_numbers("x_sq")
         x_rnorm = row_numbers("x_rnorm")
 
-        def layer_norm(g):
-            c = cols_of(g)
+        def layer_norm_factor(rows):
+            c = cols(rows)
             nc.vector.scalar_tensor_tensor(
                 out=k[:, c], in0=theta2[:, c], scalar=0.5, in1=k_rsqrt[:, c],
                 op0=ALU.mult, op1=ALU.mult,
             )
-            for i in tiles_of(g):
+
+        def layer_norm(rows):
+            for i in rows:
                 nc.vector.scalar_tensor_tensor(
                     out=x[i][:], in0=centred[i][:], scalar=k[:, i : i + 1], in1=beta_bc[:],
                     op0=ALU.mult, op1=ALU.add,
                 )
                 square_sum(x[i][:], x_sq[:, i : i + 1])
-            power(x_rnorm, x_sq, neg_half, c)
 
         bias_sq = one_number("bias_sq")
         bias_sq_clip = one_number("bias_sq_clip")
@@ -214,8 +218,10 @@ def tile_hnnlayer_s_kernel(tc, h, weight, bias, gamma, beta, out):
                 out=bias_norm[:], in0=bias_sq_clip[:], in1=half[:, 0:1], op=ALU.pow
             )
 
-        def bias_point_steps():
+        def bias_tanh_step():
             nc.scalar.activation(out=bias_tanh[:], in_=bias_norm[:], func=ACT.Tanh)
+
+        def bias_point_steps():
             nc.vector.reciprocal(out=bias_rnorm[:], in_=bias_norm[:])
             nc.vector.tensor_mul(out=y_scale[:], in0=bias_tanh[:], in1=bias_rnorm[:])
             nc.vector.tensor_scalar_mul(out=neg_y_scale[:], in0=y_scale[:], scalar1=-1.0)
@@ -266,13 +272,16 @@ def tile_hnnlayer_s_kernel(tc, h, weight, bias, gamma, beta, out):
         xt_y = row_numbers("xt_y")
         xt_norm = row_numbers("xt_norm")
 
-        def make_u(g):
-            c = cols_of(g)
+        def shrink_factor(rows):
+            c = cols(rows)
+            power(x_rnorm, x_sq, neg_half, rows)
             nc.vector.tensor_scalar(
                 out=shrink[:, c], in0=x_rnorm[:, c], scalar1=ARTANH_BOUND, scalar2=1.0,
                 op0=ALU.mult, op1=ALU.min,
             )
-            for i in tiles_of(g):
+
+        def make_u(rows):
+            for i in rows:
                 nc.vector.tensor_scalar_mul(out=u[i][:], in0=x[i][:], scalar1=shrink[:, i : i + 1])
                 u_t[i] = psum_tr.tile([P, PACK, P], BF16, name="u_t", tag="tr")
                 for t in range(PACK):
@@ -280,12 +289,12 @@ def tile_hnnlayer_s_kernel(tc, h, weight, bias, gamma, beta, out):
                         out=u_t[i][:, t, :], in_=u[i][:, t * P : (t + 1) * P], identity=ident[:]
                     )
 
-        def regroup_u(g):
-            for i in tiles_of(g):
+        def regroup_u(rows):
+            for i in rows:
                 nc.scalar.copy(out=u_grouped[i][:], in_=u_t[i][:].rearrange("p t r -> p r t"))
 
-        def multiply(g):
-            for i in tiles_of(g):
+        def multiply(rows):
+            for i in rows:
                 nc.vector.quantize_mx(
                     out=u_codes[i][:].bitcast(FP8X4),
                     scales=u_scales[i][:],
@@ -301,22 +310,23 @@ def tile_hnnlayer_s_kernel(tc, h, weight, bias, gamma, beta, out):
                     stop=True,
                 )
 
-        def row_sums(g):
-            for i in tiles_of(g):
+        def row_sums(rows):
+            for i in rows:
                 square_sum(xt[i][:], xt_sq[:, i : i + 1])
                 products = scrap.tile([P, D], F32, name="products")
                 nc.vector.scalar_tensor_tensor(
                     out=products[:], in0=xt[i][:], scalar=y_scale[:], in1=bias_bc[:],
                     op0=ALU.mult, op1=ALU.mult, accum_out=xt_y[:, i : i + 1],
                 )
-            power(xt_norm, xt_sq, half, cols_of(g))
 
         r_norm = row_numbers("r_norm")
         xt_norm_clip = row_numbers("xt_norm_clip")
         xt_rnorm = row_numbers("xt_rnorm")
         xt_y_unit2 = row_numbers("xt_y_unit2")
 
-        def exp_map(c):
+        def exp_map(rows):
+            c = cols(rows)
+            power(xt_norm, xt_sq, half, rows)
             nc.scalar.activation(out=r_norm[:, c], in_=xt_norm[:, c], func=ACT.Tanh)
             nc.vector.tensor_scalar_max(out=xt_norm_clip[:, c], in0=xt_norm[:, c], scalar1=NORM_MIN)
             nc.vector.reciprocal(out=xt_rnorm[:, c], in_=xt_norm_clip[:, c])
@@ -327,79 +337,77 @@ def tile_hnnlayer_s_kernel(tc, h, weight, bias, gamma, beta, out):
 
         r_y2 = row_numbers("r_y2")
         rho = row_numbers("rho")
-        neg_ys_r_sq = row_numbers("neg_ys_r_sq")
+        r_sq = row_numbers("r_sq")
+        y_coef = row_numbers("y_coef")
         xt_coef = row_numbers("xt_coef")
         xt_rcoef = row_numbers("xt_rcoef")
         bias_coef = row_numbers("bias_coef")
-
-        def moebius_coefficients(c):
-            nc.vector.tensor_mul(out=r_y2[:, c], in0=r_norm[:, c], in1=xt_y_unit2[:, c])
-            nc.vector.tensor_mul(out=rho[:, c], in0=r_norm[:, c], in1=xt_rnorm[:, c])
-            nc.vector.scalar_tensor_tensor(
-                out=neg_ys_r_sq[:, c], in0=r_norm[:, c], scalar=neg_y_scale[:], in1=r_norm[:, c],
-                op0=ALU.mult, op1=ALU.mult,
-            )
-            nc.vector.scalar_tensor_tensor(
-                out=xt_coef[:, c], in0=r_y2[:, c], scalar=one_plus_y_sq[:], in1=rho[:, c],
-                op0=ALU.add, op1=ALU.mult,
-            )
-            nc.vector.reciprocal(out=xt_rcoef[:, c], in_=xt_coef[:, c])
-            nc.vector.scalar_tensor_tensor(
-                out=bias_coef[:, c], in0=neg_ys_r_sq[:, c], scalar=y_scale[:], in1=xt_rcoef[:, c],
-                op0=ALU.add, op1=ALU.mult,
-            )
-
-        z = per_tile([P, D], F32, "z")
-        relu_sq = row_numbers("relu_sq")
-        relu_norm = row_numbers("relu_norm")
-
-        def direction(g):
-            for i in tiles_of(g):
-                nc.vector.scalar_tensor_tensor(
-                    out=z[i][:], in0=bias_bc[:], scalar=bias_coef[:, i : i + 1], in1=xt[i][:],
-                    op0=ALU.mult, op1=ALU.add,
-                )
-
-        def relu_square_sums(g):
-            for i in tiles_of(g):
-                products = scrap.tile([P, D], F32, name="products")
-                nc.vector.scalar_tensor_tensor(
-                    out=products[:], in0=z[i][:], scalar=0.0, in1=z[i][:],
-                    op0=ALU.max, op1=ALU.mult, accum_out=relu_sq[:, i : i + 1],
-                )
-            power(relu_norm, relu_sq, half, cols_of(g))
-
-        r_sq = row_numbers("r_sq")
         den_m1 = row_numbers("den_m1")
         den = row_numbers("den")
         sum_sq = row_numbers("sum_sq")
         sum_den = row_numbers("sum_den")
-        sum_den_clip = row_numbers("sum_den_clip")
         sum_den_rsqrt = row_numbers("sum_den_rsqrt")
         r2_norm = row_numbers("r2_norm")
         r2_clip = row_numbers("r2_clip")
 
-        def norm_of_r2(c):
+        def moebius_coefficients(rows):
+            c = cols(rows)
+            nc.vector.tensor_mul(out=r_y2[:, c], in0=r_norm[:, c], in1=xt_y_unit2[:, c])
+            nc.vector.tensor_mul(out=rho[:, c], in0=r_norm[:, c], in1=xt_rnorm[:, c])
             nc.vector.tensor_mul(out=r_sq[:, c], in0=r_norm[:, c], in1=r_norm[:, c])
+            nc.vector.scalar_tensor_tensor(
+                out=xt_coef[:, c], in0=r_y2[:, c], scalar=one_plus_y_sq[:], in1=rho[:, c],
+                op0=ALU.add, op1=ALU.mult,
+            )
+            nc.vector.tensor_scalar(
+                out=y_coef[:, c], in0=r_sq[:, c], scalar1=neg_y_scale[:], scalar2=y_scale[:],
+                op0=ALU.mult, op1=ALU.add,
+            )
             nc.vector.scalar_tensor_tensor(
                 out=den_m1[:, c], in0=r_sq[:, c], scalar=y_sq[:], in1=r_y2[:, c],
                 op0=ALU.mult, op1=ALU.add,
+            )
+            nc.vector.reciprocal(out=xt_rcoef[:, c], in_=xt_coef[:, c])
+            nc.vector.scalar_tensor_tensor(
+                out=sum_sq[:, c], in0=r_sq[:, c], scalar=y_sq[:], in1=r_y2[:, c],
+                op0=ALU.add, op1=ALU.add,
             )
             nc.vector.tensor_scalar(
                 out=den[:, c], in0=den_m1[:, c], scalar1=1.0, scalar2=NORM_MIN,
                 op0=ALU.add, op1=ALU.max,
             )
+            nc.vector.tensor_mul(out=bias_coef[:, c], in0=y_coef[:, c], in1=xt_rcoef[:, c])
+
+        def norm_of_r2(rows):
+            c = cols(rows)
             nc.vector.scalar_tensor_tensor(
-                out=sum_sq[:, c], in0=r_sq[:, c], scalar=y_sq[:], in1=r_y2[:, c],
-                op0=ALU.add, op1=ALU.add,
+                out=sum_den[:, c], in0=sum_sq[:, c], scalar=SUM_SQ_MIN, in1=den[:, c],
+                op0=ALU.max, op1=ALU.mult,
             )
-            nc.vector.tensor_mul(out=sum_den[:, c], in0=sum_sq[:, c], in1=den[:, c])
-            nc.vector.tensor_scalar_max(out=sum_den_clip[:, c], in0=sum_den[:, c], scalar1=NORM_MIN_SQ)
-            power(sum_den_rsqrt, sum_den_clip, neg_half, c)
+            power(sum_den_rsqrt, sum_den, neg_half, rows)
             nc.gpsimd.tensor_tensor(
                 out=r2_norm[:, c], in0=sum_sq[:, c], in1=sum_den_rsqrt[:, c], op=ALU.mult
             )
             nc.gpsimd.tensor_scalar_min(out=r2_clip[:, c], in0=r2_norm[:, c], scalar1=BOUND)
+
+        z = per_tile([P, D], F32, "z")
+        relu_sq = row_numbers("relu_sq")
+        relu_norm = row_numbers("relu_norm")
+
+        def direction(rows):
+            for i in rows:
+                nc.vector.scalar_tensor_tensor(
+                    out=z[i][:], in0=bias_bc[:], scalar=bias_coef[:, i : i + 1], in1=xt[i][:],
+                    op0=ALU.mult, op1=ALU.add,
+                )
+
+        def relu_square_sums(rows):
+            for i in rows:
+                products = scrap.tile([P, D], F32, name="products")
+                nc.vector.scalar_tensor_tensor(
+                    out=products[:], in0=z[i][:], scalar=0.0, in1=z[i][:],
+                    op0=ALU.max, op1=ALU.mult, accum_out=relu_sq[:, i : i + 1],
+                )
 
         ln_up2 = row_numbers("ln_up2")
         ln_dn2 = row_numbers("ln_dn2")
@@ -407,11 +415,13 @@ def tile_hnnlayer_s_kernel(tc, h, weight, bias, gamma, beta, out):
         artanh2 = row_numbers("artanh2")
         log_coef = row_numbers("log_coef")
 
-        def log_of_r2(c):
+        def log_of_r2(rows):
+            c = cols(rows)
             nc.scalar.activation(out=ln_up2[:, c], in_=r2_clip[:, c], func=ACT.Ln, bias=1.0, scale=1.0)
             nc.scalar.activation(out=ln_dn2[:, c], in_=r2_clip[:, c], func=ACT.Ln, bias=1.0, scale=-1.0)
 
-        def log_map_coefficient(c):
+        def log_map_coefficient(rows):
+            c = cols(rows)
             nc.vector.tensor_mul(out=z_unit[:, c], in0=xt_coef[:, c], in1=sum_den_rsqrt[:, c])
             nc.vector.tensor_sub(out=artanh2[:, c], in0=ln_up2[:, c], in1=ln_dn2[:, c])
             nc.vector.scalar_tensor_tensor(
@@ -426,7 +436,9 @@ def tile_hnnlayer_s_kernel(tc, h, weight, bias, gamma, beta, out):
         out_coef = row_numbers("out_coef")
         result = per_tile([P, D], F32, "result")
 
-        def out_coefficient(c):
+        def out_coefficient(rows):
+            c = cols(rows)
+            power(relu_norm, relu_sq, half, rows)
             nc.vector.scalar_tensor_tensor(
                 out=v_norm[:, c], in0=relu_norm[:, c], scalar=NORM_MIN, in1=log_coef[:, c],
                 op0=ALU.max, op1=ALU.mult,
@@ -436,8 +448,8 @@ def tile_hnnlayer_s_kernel(tc, h, weight, bias, gamma, beta, out):
             nc.vector.reciprocal(out=relu_rnorm[:, c], in_=relu_norm_clip[:, c])
             nc.vector.tensor_mul(out=out_coef[:, c], in0=v_tanh[:, c], in1=relu_rnorm[:, c])
 
-        def finish(g):
-            for i in tiles_of(g):
+        def finish(rows):
+            for i in rows:
                 if i % 2 == 0:
                     nc.scalar.activation(
                         out=result[i][:], in_=z[i][:], func=ACT.Relu, scale=out_coef[:, i : i + 1]
@@ -449,42 +461,50 @@ def tile_hnnlayer_s_kernel(tc, h, weight, bias, gamma, beta, out):
                     )
                 nc.sync.dma_start(out=out[i * P : (i + 1) * P, :], in_=result[i][:])
 
+        ALL = range(TILES)
+        PAIRS = [range(0, 2), range(2, 4)]
+        SINGLES = [range(i, i + 1) for i in range(TILES)]
+
         transpose_weight()
-        shifted_sums(0)
-        shifted_sums(1)
+        shifted_sums(range(0, 3))
+        first_terms(ALL)
+        shifted_sums(range(3, 4))
         norm_of_h(ALL)
-        centre(0)
+        centre(PAIRS[0])
         log_of_h(ALL)
         variance(ALL)
-        centre(1)
+        centre(PAIRS[1])
         bias_square_sum()
-        layer_norm_scale(ALL)
         bias_norm_steps()
+        layer_norm_scale(ALL)
+        bias_tanh_step()
         regroup_weight(0)
         regroup_weight(1)
-        layer_norm(0)
-        layer_norm(1)
-        quantise_weight()
-        make_u(0)
         bias_point_steps()
-        regroup_u(0)
-        make_u(1)
-        multiply(0)
-        regroup_u(1)
-        row_sums(0)
-        multiply(1)
-        row_sums(1)
+        layer_norm_factor(ALL)
+        layer_norm(ALL)
+        quantise_weight()
+        for rows in PAIRS:
+            shrink_factor(rows)
+            make_u(rows)
+        for rows in SINGLES:
+            regroup_u(rows)
+        for rows in SINGLES:
+            multiply(rows)
+        for rows in SINGLES:
+            row_sums(rows)
         exp_map(ALL)
         moebius_coefficients(ALL)
         load_table(ACT.Ln, "warm_ln_b")
+        direction(SINGLES[0])
         norm_of_r2(ALL)
-        direction(0)
-        direction(1)
+        direction(range(1, 4))
         log_of_r2(ALL)
         load_table(ACT.Tanh, "warm_tanh_b")
-        relu_square_sums(0)
+        relu_square_sums(PAIRS[0])
         log_map_coefficient(ALL)
-        relu_square_sums(1)
-        out_coefficient(ALL)
-        finish(0)
-        finish(1)
+        out_coefficient(PAIRS[0])
+        relu_square_sums(PAIRS[1])
+        finish(PAIRS[0])
+        out_coefficient(PAIRS[1])
+        finish(PAIRS[1])

@@ -391,7 +391,7 @@ def tile_hnnlayer_s_kernel(tc, h, weight, bias, gamma, beta, out):
             nc.gpsimd.tensor_scalar_min(out=r2_clip[:, c], in0=r2_norm[:, c], scalar1=BOUND)
 
         z = per_tile([P, D], F32, "z")
-        relu_sq = row_numbers("relu_sq")
+        relu_sq = keep.tile([P, 2, 8], F32, name="relu_sq")
         relu_norm = row_numbers("relu_norm")
 
         def direction(rows):
@@ -406,8 +406,14 @@ def tile_hnnlayer_s_kernel(tc, h, weight, bias, gamma, beta, out):
                 products = scrap.tile([P, D], F32, name="products")
                 nc.vector.scalar_tensor_tensor(
                     out=products[:], in0=z[i][:], scalar=0.0, in1=z[i][:],
-                    op0=ALU.max, op1=ALU.mult, accum_out=relu_sq[:, i : i + 1],
+                    op0=ALU.max, op1=ALU.mult, accum_out=relu_sq[:, i // 2, i % 2 : i % 2 + 1],
                 )
+
+        def relu_square_sums_on_scalar(rows):
+            for i in rows:
+                relu_z = scrap.tile([P, D], F32, name="relu_z")
+                nc.scalar.activation(out=relu_z[:], in_=z[i][:], func=ACT.Relu)
+                square_sum(relu_z[:], relu_sq[:, i // 2, i % 2 : i % 2 + 1])
 
         ln_up2 = row_numbers("ln_up2")
         ln_dn2 = row_numbers("ln_dn2")
@@ -438,7 +444,12 @@ def tile_hnnlayer_s_kernel(tc, h, weight, bias, gamma, beta, out):
 
         def out_coefficient(rows):
             c = cols(rows)
-            power(relu_norm, relu_sq, half, rows)
+            nc.gpsimd.tensor_tensor(
+                out=relu_norm[:].rearrange("p (a b) -> p a b", a=2),
+                in0=relu_sq[:, :, 0:2],
+                in1=half[:].rearrange("p (a b) -> p a b", a=2),
+                op=ALU.pow,
+            )
             nc.vector.scalar_tensor_tensor(
                 out=v_norm[:, c], in0=relu_norm[:, c], scalar=NORM_MIN, in1=log_coef[:, c],
                 op0=ALU.max, op1=ALU.mult,
@@ -499,12 +510,10 @@ def tile_hnnlayer_s_kernel(tc, h, weight, bias, gamma, beta, out):
         direction(SINGLES[0])
         norm_of_r2(ALL)
         direction(range(1, 4))
+        relu_square_sums_on_scalar(PAIRS[0])
         log_of_r2(ALL)
         load_table(ACT.Tanh, "warm_tanh_b")
-        relu_square_sums(PAIRS[0])
-        log_map_coefficient(ALL)
-        out_coefficient(PAIRS[0])
         relu_square_sums(PAIRS[1])
-        finish(PAIRS[0])
-        out_coefficient(PAIRS[1])
-        finish(PAIRS[1])
+        log_map_coefficient(ALL)
+        out_coefficient(ALL)
+        finish(ALL)

@@ -67,6 +67,8 @@ def tile_hnnlayer_s_kernel(tc, h, weight, bias, gamma, beta, out):
         h_sb = keep.tile([P, TILES, D], BF16, name="h_sb")
         for i in range(TILES):
             nc.sync.dma_start(out=h_sb[:, i, :], in_=h[i * P : (i + 1) * P, :])
+        w_sb = keep.tile([P, TILES, D], BF16, name="w_sb")
+        nc.sync.dma_start(out=w_sb[:], in_=weight.rearrange("(o p) k -> p o k", p=P))
         gamma_bc = keep.tile([P, D], BF16, name="gamma_bc")
         nc.sync.dma_start(out=gamma_bc[:], in_=gamma.partition_broadcast(P))
         bias_bc = keep.tile([P, D], BF16, name="bias_bc")
@@ -75,8 +77,6 @@ def tile_hnnlayer_s_kernel(tc, h, weight, bias, gamma, beta, out):
         )
         beta_bc = keep.tile([P, D], BF16, name="beta_bc")
         nc.sync.dma_start(out=beta_bc[:], in_=beta.partition_broadcast(P))
-        w_sb = keep.tile([P, TILES, D], BF16, name="w_sb")
-        nc.sync.dma_start(out=w_sb[:], in_=weight.rearrange("(o p) k -> p o k", p=P))
 
         half = row_numbers("half")
         nc.vector.memset(half[:], 0.5)
@@ -143,6 +143,7 @@ def tile_hnnlayer_s_kernel(tc, h, weight, bias, gamma, beta, out):
         d_sum_mean = row_numbers("d_sum_mean")
         dev_sq = row_numbers("dev_sq")
         eps_h_sq = row_numbers("eps_h_sq")
+        quarter_var = row_numbers("quarter_var")
 
         def variance(rows):
             c = cols(rows)
@@ -152,6 +153,7 @@ def tile_hnnlayer_s_kernel(tc, h, weight, bias, gamma, beta, out):
                 out=eps_h_sq[:, c], in0=h_sq[:, c], scalar1=NORM_MIN_SQ, scalar2=LN_EPS,
                 op0=ALU.max, op1=ALU.mult,
             )
+            nc.vector.tensor_scalar_mul(out=quarter_var[:, c], in0=dev_sq[:, c], scalar1=0.25 / D)
 
         ln_up = row_numbers("ln_up")
         ln_dn = row_numbers("ln_dn")
@@ -163,21 +165,24 @@ def tile_hnnlayer_s_kernel(tc, h, weight, bias, gamma, beta, out):
 
         theta2 = row_numbers("theta2")
         theta_sq = row_numbers("theta_sq")
-        theta_sq_var = row_numbers("theta_sq_var")
         k_arg = row_numbers("k_arg")
         k_rsqrt = row_numbers("k_rsqrt")
         k = row_numbers("k")
 
         def layer_norm_scale(rows):
             c = cols(rows)
-            nc.vector.tensor_sub(out=theta2[:, c], in0=ln_up[:, c], in1=ln_dn[:, c])
-            nc.vector.scalar_tensor_tensor(
-                out=theta_sq[:, c], in0=theta2[:, c], scalar=0.25 / D, in1=theta2[:, c],
-                op0=ALU.mult, op1=ALU.mult,
-            )
-            nc.vector.tensor_mul(out=theta_sq_var[:, c], in0=theta_sq[:, c], in1=dev_sq[:, c])
-            nc.vector.tensor_add(out=k_arg[:, c], in0=theta_sq_var[:, c], in1=eps_h_sq[:, c])
+            for i in rows:
+                nc.scalar.activation(
+                    out=theta_sq[:, i : i + 1], in_=ln_dn[:, i : i + 1], func=ACT.Square,
+                    scale=-1.0, bias=ln_up[:, i : i + 1],
+                )
+            for i in rows:
+                nc.scalar.activation(
+                    out=k_arg[:, i : i + 1], in_=theta_sq[:, i : i + 1], func=ACT.Identity,
+                    scale=quarter_var[:, i : i + 1], bias=eps_h_sq[:, i : i + 1],
+                )
             power(k_rsqrt, k_arg, neg_half, rows)
+            nc.vector.tensor_sub(out=theta2[:, c], in0=ln_up[:, c], in1=ln_dn[:, c])
 
         x = per_tile([P, D], F32, "x")
         x_sq = row_numbers("x_sq")
@@ -461,7 +466,7 @@ def tile_hnnlayer_s_kernel(tc, h, weight, bias, gamma, beta, out):
 
         def finish(rows):
             for i in rows:
-                if i % 2 == 0:
+                if i == TILES - 1:
                     nc.scalar.activation(
                         out=result[i][:], in_=z[i][:], func=ACT.Relu, scale=out_coef[:, i : i + 1]
                     )
@@ -481,29 +486,26 @@ def tile_hnnlayer_s_kernel(tc, h, weight, bias, gamma, beta, out):
         first_terms(ALL)
         shifted_sums(range(3, 4))
         norm_of_h(ALL)
+        regroup_weight(0)
         centre(PAIRS[0])
-        log_of_h(ALL)
         variance(ALL)
+        log_of_h(ALL)
+        layer_norm_scale(ALL)
         centre(PAIRS[1])
         bias_square_sum()
         bias_norm_steps()
-        layer_norm_scale(ALL)
         bias_tanh_step()
-        regroup_weight(0)
-        regroup_weight(1)
-        bias_point_steps()
         layer_norm_factor(ALL)
         layer_norm(ALL)
-        quantise_weight()
+        regroup_weight(1)
+        bias_point_steps()
         for rows in PAIRS:
             shrink_factor(rows)
             make_u(rows)
-        for rows in SINGLES:
-            regroup_u(rows)
-        for rows in SINGLES:
-            multiply(rows)
-        for rows in SINGLES:
-            row_sums(rows)
+        quantise_weight()
+        regroup_u(ALL)
+        multiply(ALL)
+        row_sums(ALL)
         exp_map(ALL)
         moebius_coefficients(ALL)
         load_table(ACT.Ln, "warm_ln_b")

@@ -22,7 +22,7 @@ BOUND = 1.0 - 168.0 * 2.0 ** -24
 ARTANH_BOUND = 0.5 * math.log((1.0 + BOUND) / (1.0 - BOUND))
 LN_EPS = 1e-5
 NORM_MIN = 1e-15
-NORM_MIN_SQ = 1e-30
+NORM_MIN_SQ = NORM_MIN * NORM_MIN
 SUM_SQ_MIN = 1e-20
 
 FLOPS = 2 * N_ROWS * D * D
@@ -86,23 +86,23 @@ def tile_hnnlayer_s_kernel(tc, h, weight, bias, gamma, beta, out):
         nc.vector.memset(ones[:], 1.0)
         ident = keep.tile([P, P], BF16, name="ident")
         make_identity(nc, ident[:])
-        load_table(ACT.Ln, "warm_ln_a")
+        load_table(ACT.Ln, "table_ln_1")
 
         first = h_sb[:, :, 0]
-        d = per_tile([P, D], F32, "d")
-        d_sum = row_numbers("d_sum")
-        d_sq = row_numbers("d_sq")
+        shifted = per_tile([P, D], F32, "shifted")
+        shifted_sum = row_numbers("shifted_sum")
+        shifted_sq = row_numbers("shifted_sq")
 
         def shifted_sums(rows):
             for i in rows:
                 squares = scrap.tile([P, D], BF16, name="squares")
                 nc.scalar.activation(
                     out=squares[:], in_=h_sb[:, i, :], func=ACT.Square, scale=-1.0,
-                    bias=h_sb[:, i, 0:1], accum_out=d_sq[:, i : i + 1],
+                    bias=h_sb[:, i, 0:1], accum_out=shifted_sq[:, i : i + 1],
                 )
                 nc.vector.tensor_scalar(
-                    out=d[i][:], in0=h_sb[:, i, :], scalar1=h_sb[:, i, 0:1], scalar2=None,
-                    op0=ALU.subtract, op1=ALU.add, accum_out=d_sum[:, i : i + 1],
+                    out=shifted[i][:], in0=h_sb[:, i, :], scalar1=h_sb[:, i, 0:1], scalar2=None,
+                    op0=ALU.subtract, op1=ALU.add, accum_out=shifted_sum[:, i : i + 1],
                 )
 
         first_x2 = row_numbers("first_x2")
@@ -112,43 +112,47 @@ def tile_hnnlayer_s_kernel(tc, h, weight, bias, gamma, beta, out):
         h_sq = row_numbers("h_sq")
         h_norm = row_numbers("h_norm")
         h_clip = row_numbers("h_clip")
-        d_mean = row_numbers("d_mean")
+        shifted_mean = row_numbers("shifted_mean")
 
         def first_terms(rows):
             c = cols(rows)
             nc.vector.tensor_scalar_mul(out=first_x2[:, c], in0=first[:, c], scalar1=2.0)
             nc.vector.scalar_tensor_tensor(
-                out=first_sq[:, c], in0=first[:, c], scalar=1.0 * D, in1=first[:, c],
+                out=first_sq[:, c], in0=first[:, c], scalar=float(D), in1=first[:, c],
                 op0=ALU.mult, op1=ALU.mult,
             )
 
         def norm_of_h(rows):
             c = cols(rows)
-            nc.vector.tensor_add(out=h_sq_a[:, c], in0=d_sq[:, c], in1=first_sq[:, c])
-            nc.vector.tensor_mul(out=h_sq_b[:, c], in0=d_sum[:, c], in1=first_x2[:, c])
+            nc.vector.tensor_add(out=h_sq_a[:, c], in0=shifted_sq[:, c], in1=first_sq[:, c])
+            nc.vector.tensor_mul(out=h_sq_b[:, c], in0=shifted_sum[:, c], in1=first_x2[:, c])
             nc.vector.tensor_add(out=h_sq[:, c], in0=h_sq_a[:, c], in1=h_sq_b[:, c])
             power(h_norm, h_sq, half, rows)
             nc.gpsimd.tensor_scalar_min(out=h_clip[:, c], in0=h_norm[:, c], scalar1=BOUND)
-            nc.vector.tensor_scalar_mul(out=d_mean[:, c], in0=d_sum[:, c], scalar1=1.0 / D)
+            nc.vector.tensor_scalar_mul(
+                out=shifted_mean[:, c], in0=shifted_sum[:, c], scalar1=1.0 / D
+            )
 
         centred = per_tile([P, D], F32, "centred")
 
         def centre(rows):
             for i in rows:
                 nc.vector.scalar_tensor_tensor(
-                    out=centred[i][:], in0=d[i][:], scalar=d_mean[:, i : i + 1],
+                    out=centred[i][:], in0=shifted[i][:], scalar=shifted_mean[:, i : i + 1],
                     in1=gamma_bc[:], op0=ALU.subtract, op1=ALU.mult,
                 )
 
-        d_sum_mean = row_numbers("d_sum_mean")
+        mean_part = row_numbers("mean_part")
         dev_sq = row_numbers("dev_sq")
         eps_h_sq = row_numbers("eps_h_sq")
         quarter_var = row_numbers("quarter_var")
 
         def variance(rows):
             c = cols(rows)
-            nc.vector.tensor_mul(out=d_sum_mean[:, c], in0=d_sum[:, c], in1=d_mean[:, c])
-            nc.vector.tensor_sub(out=dev_sq[:, c], in0=d_sq[:, c], in1=d_sum_mean[:, c])
+            nc.vector.tensor_mul(
+                out=mean_part[:, c], in0=shifted_sum[:, c], in1=shifted_mean[:, c]
+            )
+            nc.vector.tensor_sub(out=dev_sq[:, c], in0=shifted_sq[:, c], in1=mean_part[:, c])
             nc.vector.tensor_scalar(
                 out=eps_h_sq[:, c], in0=h_sq[:, c], scalar1=NORM_MIN_SQ, scalar2=LN_EPS,
                 op0=ALU.max, op1=ALU.mult,
@@ -160,46 +164,50 @@ def tile_hnnlayer_s_kernel(tc, h, weight, bias, gamma, beta, out):
 
         def log_of_h(rows):
             c = cols(rows)
-            nc.scalar.activation(out=ln_up[:, c], in_=h_clip[:, c], func=ACT.Ln, bias=1.0, scale=1.0)
-            nc.scalar.activation(out=ln_dn[:, c], in_=h_clip[:, c], func=ACT.Ln, bias=1.0, scale=-1.0)
+            nc.scalar.activation(
+                out=ln_up[:, c], in_=h_clip[:, c], func=ACT.Ln, bias=1.0, scale=1.0
+            )
+            nc.scalar.activation(
+                out=ln_dn[:, c], in_=h_clip[:, c], func=ACT.Ln, bias=1.0, scale=-1.0
+            )
 
         theta2 = row_numbers("theta2")
-        theta_sq = row_numbers("theta_sq")
-        k_arg = row_numbers("k_arg")
-        k_rsqrt = row_numbers("k_rsqrt")
-        k = row_numbers("k")
+        theta2_sq = row_numbers("theta2_sq")
+        factor_arg = row_numbers("factor_arg")
+        factor_rsqrt = row_numbers("factor_rsqrt")
+        ln_factor = row_numbers("ln_factor")
 
-        def layer_norm_scale(rows):
+        def layer_norm_factor_argument(rows):
             c = cols(rows)
             for i in rows:
                 nc.scalar.activation(
-                    out=theta_sq[:, i : i + 1], in_=ln_dn[:, i : i + 1], func=ACT.Square,
+                    out=theta2_sq[:, i : i + 1], in_=ln_dn[:, i : i + 1], func=ACT.Square,
                     scale=-1.0, bias=ln_up[:, i : i + 1],
                 )
             for i in rows:
                 nc.scalar.activation(
-                    out=k_arg[:, i : i + 1], in_=theta_sq[:, i : i + 1], func=ACT.Identity,
+                    out=factor_arg[:, i : i + 1], in_=theta2_sq[:, i : i + 1], func=ACT.Identity,
                     scale=quarter_var[:, i : i + 1], bias=eps_h_sq[:, i : i + 1],
                 )
-            power(k_rsqrt, k_arg, neg_half, rows)
+            power(factor_rsqrt, factor_arg, neg_half, rows)
             nc.vector.tensor_sub(out=theta2[:, c], in0=ln_up[:, c], in1=ln_dn[:, c])
+
+        def layer_norm_factor(rows):
+            c = cols(rows)
+            nc.vector.scalar_tensor_tensor(
+                out=ln_factor[:, c], in0=theta2[:, c], scalar=0.5, in1=factor_rsqrt[:, c],
+                op0=ALU.mult, op1=ALU.mult,
+            )
 
         x = per_tile([P, D], F32, "x")
         x_sq = row_numbers("x_sq")
         x_rnorm = row_numbers("x_rnorm")
 
-        def layer_norm_factor(rows):
-            c = cols(rows)
-            nc.vector.scalar_tensor_tensor(
-                out=k[:, c], in0=theta2[:, c], scalar=0.5, in1=k_rsqrt[:, c],
-                op0=ALU.mult, op1=ALU.mult,
-            )
-
         def layer_norm(rows):
             for i in rows:
                 nc.vector.scalar_tensor_tensor(
-                    out=x[i][:], in0=centred[i][:], scalar=k[:, i : i + 1], in1=beta_bc[:],
-                    op0=ALU.mult, op1=ALU.add,
+                    out=x[i][:], in0=centred[i][:], scalar=ln_factor[:, i : i + 1],
+                    in1=beta_bc[:], op0=ALU.mult, op1=ALU.add,
                 )
                 square_sum(x[i][:], x_sq[:, i : i + 1])
 
@@ -215,18 +223,18 @@ def tile_hnnlayer_s_kernel(tc, h, weight, bias, gamma, beta, out):
 
         def bias_square_sum():
             square_sum(bias_bc[:], bias_sq[:])
-            load_table(ACT.Tanh, "warm_tanh_a")
+            load_table(ACT.Tanh, "table_tanh_1")
 
-        def bias_norm_steps():
+        def norm_of_bias():
             nc.vector.tensor_scalar_max(out=bias_sq_clip[:], in0=bias_sq[:], scalar1=NORM_MIN_SQ)
             nc.gpsimd.tensor_tensor(
                 out=bias_norm[:], in0=bias_sq_clip[:], in1=half[:, 0:1], op=ALU.pow
             )
 
-        def bias_tanh_step():
+        def tanh_of_bias():
             nc.scalar.activation(out=bias_tanh[:], in_=bias_norm[:], func=ACT.Tanh)
 
-        def bias_point_steps():
+        def bias_point():
             nc.vector.reciprocal(out=bias_rnorm[:], in_=bias_norm[:])
             nc.vector.tensor_mul(out=y_scale[:], in0=bias_tanh[:], in1=bias_rnorm[:])
             nc.vector.tensor_scalar_mul(out=neg_y_scale[:], in0=y_scale[:], scalar1=-1.0)
@@ -236,10 +244,10 @@ def tile_hnnlayer_s_kernel(tc, h, weight, bias, gamma, beta, out):
             )
             nc.vector.tensor_scalar_add(out=one_plus_y_sq[:], in0=y_sq[:], scalar1=1.0)
 
+        w_t = [psum_tr.tile([P, 2, PACK, P], BF16, name="w_t%d" % b, tag="tr") for b in range(2)]
         w_grouped = keep.tile([P, D, PACK], BF16, name="w_grouped", align_bytes=64)
         w_codes = keep.tile([P, D], U32, name="w_codes", align_bytes=64)
         w_scales = keep.tile([P, D], U8, name="w_scales", align_bytes=64)
-        w_t = [psum_tr.tile([P, 2, PACK, P], BF16, name="w_t%d" % b, tag="tr") for b in range(2)]
 
         def transpose_weight():
             for b in range(2):
@@ -263,7 +271,7 @@ def tile_hnnlayer_s_kernel(tc, h, weight, bias, gamma, beta, out):
             nc.vector.quantize_mx(
                 out=w_codes[:].bitcast(FP8X4),
                 scales=w_scales[:],
-                in_=w_grouped[:].rearrange("p c t -> p (c t)"),
+                in_=w_grouped[:].rearrange("p o t -> p (o t)"),
             )
 
         shrink = row_numbers("shrink")
@@ -406,7 +414,7 @@ def tile_hnnlayer_s_kernel(tc, h, weight, bias, gamma, beta, out):
                     op0=ALU.mult, op1=ALU.add,
                 )
 
-        def relu_square_sums(rows):
+        def relu_square_sums_on_vector(rows):
             for i in rows:
                 products = scrap.tile([P, D], F32, name="products")
                 nc.vector.scalar_tensor_tensor(
@@ -428,8 +436,12 @@ def tile_hnnlayer_s_kernel(tc, h, weight, bias, gamma, beta, out):
 
         def log_of_r2(rows):
             c = cols(rows)
-            nc.scalar.activation(out=ln_up2[:, c], in_=r2_clip[:, c], func=ACT.Ln, bias=1.0, scale=1.0)
-            nc.scalar.activation(out=ln_dn2[:, c], in_=r2_clip[:, c], func=ACT.Ln, bias=1.0, scale=-1.0)
+            nc.scalar.activation(
+                out=ln_up2[:, c], in_=r2_clip[:, c], func=ACT.Ln, bias=1.0, scale=1.0
+            )
+            nc.scalar.activation(
+                out=ln_dn2[:, c], in_=r2_clip[:, c], func=ACT.Ln, bias=1.0, scale=-1.0
+            )
 
         def log_map_coefficient(rows):
             c = cols(rows)
@@ -447,8 +459,7 @@ def tile_hnnlayer_s_kernel(tc, h, weight, bias, gamma, beta, out):
         out_coef = row_numbers("out_coef")
         result = per_tile([P, D], F32, "result")
 
-        def out_coefficient(rows):
-            c = cols(rows)
+        def out_coefficient():
             nc.gpsimd.tensor_tensor(
                 out=relu_norm[:].rearrange("p (a b) -> p a b", a=2),
                 in0=relu_sq[:, :, 0:2],
@@ -456,13 +467,13 @@ def tile_hnnlayer_s_kernel(tc, h, weight, bias, gamma, beta, out):
                 op=ALU.pow,
             )
             nc.vector.scalar_tensor_tensor(
-                out=v_norm[:, c], in0=relu_norm[:, c], scalar=NORM_MIN, in1=log_coef[:, c],
+                out=v_norm[:], in0=relu_norm[:], scalar=NORM_MIN, in1=log_coef[:],
                 op0=ALU.max, op1=ALU.mult,
             )
-            nc.scalar.activation(out=v_tanh[:, c], in_=v_norm[:, c], func=ACT.Tanh)
-            nc.vector.tensor_scalar_max(out=relu_norm_clip[:, c], in0=relu_norm[:, c], scalar1=NORM_MIN)
-            nc.vector.reciprocal(out=relu_rnorm[:, c], in_=relu_norm_clip[:, c])
-            nc.vector.tensor_mul(out=out_coef[:, c], in0=v_tanh[:, c], in1=relu_rnorm[:, c])
+            nc.scalar.activation(out=v_tanh[:], in_=v_norm[:], func=ACT.Tanh)
+            nc.vector.tensor_scalar_max(out=relu_norm_clip[:], in0=relu_norm[:], scalar1=NORM_MIN)
+            nc.vector.reciprocal(out=relu_rnorm[:], in_=relu_norm_clip[:])
+            nc.vector.tensor_mul(out=out_coef[:], in0=v_tanh[:], in1=relu_rnorm[:])
 
         def finish(rows):
             for i in rows:
@@ -478,28 +489,28 @@ def tile_hnnlayer_s_kernel(tc, h, weight, bias, gamma, beta, out):
                 nc.sync.dma_start(out=out[i * P : (i + 1) * P, :], in_=result[i][:])
 
         ALL = range(TILES)
-        PAIRS = [range(0, 2), range(2, 4)]
-        SINGLES = [range(i, i + 1) for i in range(TILES)]
+        FIRST_PAIR = range(0, 2)
+        LAST_PAIR = range(2, 4)
 
         transpose_weight()
-        shifted_sums(range(0, 3))
+        shifted_sums(range(0, TILES - 1))
         first_terms(ALL)
-        shifted_sums(range(3, 4))
+        shifted_sums(range(TILES - 1, TILES))
         norm_of_h(ALL)
         regroup_weight(0)
-        centre(PAIRS[0])
+        centre(FIRST_PAIR)
         variance(ALL)
         log_of_h(ALL)
-        layer_norm_scale(ALL)
-        centre(PAIRS[1])
+        layer_norm_factor_argument(ALL)
+        centre(LAST_PAIR)
         bias_square_sum()
-        bias_norm_steps()
-        bias_tanh_step()
+        norm_of_bias()
+        tanh_of_bias()
         layer_norm_factor(ALL)
         layer_norm(ALL)
         regroup_weight(1)
-        bias_point_steps()
-        for rows in PAIRS:
+        bias_point()
+        for rows in (FIRST_PAIR, LAST_PAIR):
             shrink_factor(rows)
             make_u(rows)
         quantise_weight()
@@ -508,14 +519,14 @@ def tile_hnnlayer_s_kernel(tc, h, weight, bias, gamma, beta, out):
         row_sums(ALL)
         exp_map(ALL)
         moebius_coefficients(ALL)
-        load_table(ACT.Ln, "warm_ln_b")
-        direction(SINGLES[0])
+        load_table(ACT.Ln, "table_ln_2")
+        direction(range(0, 1))
         norm_of_r2(ALL)
-        direction(range(1, 4))
-        relu_square_sums_on_scalar(PAIRS[0])
+        direction(range(1, TILES))
+        relu_square_sums_on_scalar(FIRST_PAIR)
         log_of_r2(ALL)
-        load_table(ACT.Tanh, "warm_tanh_b")
-        relu_square_sums(PAIRS[1])
+        load_table(ACT.Tanh, "table_tanh_2")
+        relu_square_sums_on_vector(LAST_PAIR)
         log_map_coefficient(ALL)
-        out_coefficient(ALL)
+        out_coefficient()
         finish(ALL)

import math
from contextlib import ExitStack

import concourse.mybir as mybir
from concourse.masks import make_identity

F32 = mybir.dt.float32
BF16 = mybir.dt.bfloat16
U32 = mybir.dt.uint32
U8 = mybir.dt.uint8
FP8X4 = mybir.dt.float8_e4m3fn_x4
ALU = mybir.AluOpType
ACT = mybir.ActivationFunctionType

P = 128
PACK = 4
N_ROWS = 512
D = 512
TILES = N_ROWS // P

BOUND = 1.0 - 168.0 * 2.0 ** -24
ARTANH_BOUND = 0.5 * math.log((1.0 + BOUND) / (1.0 - BOUND))
LN_EPS = 1e-5
NORM_MIN = 1e-15
NORM_MIN_SQ = NORM_MIN * NORM_MIN
SUM_SQ_MIN = 1e-20

FLOPS = 2 * N_ROWS * D * D


def tile_hnnlayer_s_kernel(tc, h, weight, bias, gamma, beta, out):
    nc = tc.nc
    with ExitStack() as ctx:
        keep = ctx.enter_context(tc.tile_pool(name="keep", bufs=1))
        scrap = ctx.enter_context(tc.tile_pool(name="scrap", bufs=4))
        psum_tr = ctx.enter_context(tc.psum_pool(name="psum_tr", bufs=4))
        psum_xt = ctx.enter_context(tc.psum_pool(name="psum_xt", bufs=1))
        ctx.enter_context(tc.manual_schedule())

        def per_tile(shape, dtype, name):
            return [
                keep.tile(shape, dtype, name="%s%d" % (name, i), align_bytes=64)
                for i in range(TILES)
            ]

        def row_numbers(name):
            return keep.tile([P, TILES], F32, name=name)

        def one_number(name):
            return keep.tile([P, 1], F32, name=name)

        def cols(rows):
            return slice(rows[0], rows[-1] + 1)

        def power(dst, src, exponent, rows):
            c = cols(rows)
            nc.gpsimd.tensor_tensor(out=dst[:, c], in0=src[:, c], in1=exponent[:, c], op=ALU.pow)

        def load_table(func, name):
            unused = one_number(name)
            nc.scalar.activation(out=unused[:], in_=ones[:], func=func)

        def square_sum(src, total):
            squares = scrap.tile([P, D], BF16, name="squares")
            nc.scalar.activation(out=squares[:], in_=src, func=ACT.Square, accum_out=total)

        h_sb = keep.tile([P, TILES, D], BF16, name="h_sb")
        for i in range(TILES):
            nc.sync.dma_start(out=h_sb[:, i, :], in_=h[i * P : (i + 1) * P, :])
        w_sb = keep.tile([P, TILES, D], BF16, name="w_sb")
        nc.sync.dma_start(out=w_sb[:], in_=weight.rearrange("(o p) k -> p o k", p=P))
        gamma_bc = keep.tile([P, D], BF16, name="gamma_bc")
        nc.sync.dma_start(out=gamma_bc[:], in_=gamma.partition_broadcast(P))
        bias_bc = keep.tile([P, D], BF16, name="bias_bc")
        nc.sync.dma_start(
            out=bias_bc[:], in_=bias.rearrange("o d -> (o d)").partition_broadcast(P)
        )
        beta_bc = keep.tile([P, D], BF16, name="beta_bc")
        nc.sync.dma_start(out=beta_bc[:], in_=beta.partition_broadcast(P))

        half = row_numbers("half")
        nc.vector.memset(half[:], 0.5)
        neg_half = row_numbers("neg_half")
        nc.vector.memset(neg_half[:], -0.5)
        ones = one_number("ones")
        nc.vector.memset(ones[:], 1.0)
        ident = keep.tile([P, P], BF16, name="ident")
        make_identity(nc, ident[:])
        load_table(ACT.Ln, "table_ln_1")

        first = h_sb[:, :, 0]
        shifted = per_tile([P, D], F32, "shifted")
        shifted_sum = row_numbers("shifted_sum")
        shifted_sq = row_numbers("shifted_sq")

        def shifted_sums(rows):
            for i in rows:
                squares = scrap.tile([P, D], BF16, name="squares")
                nc.scalar.activation(
                    out=squares[:], in_=h_sb[:, i, :], func=ACT.Square, scale=-1.0,
                    bias=h_sb[:, i, 0:1], accum_out=shifted_sq[:, i : i + 1],
                )
                nc.vector.tensor_scalar(
                    out=shifted[i][:], in0=h_sb[:, i, :], scalar1=h_sb[:, i, 0:1], scalar2=None,
                    op0=ALU.subtract, op1=ALU.add, accum_out=shifted_sum[:, i : i + 1],
                )

        first_x2 = row_numbers("first_x2")
        first_sq = row_numbers("first_sq")
        h_sq_a = row_numbers("h_sq_a")
        h_sq_b = row_numbers("h_sq_b")
        h_sq = row_numbers("h_sq")
        h_norm = row_numbers("h_norm")
        h_clip = row_numbers("h_clip")
        shifted_mean = row_numbers("shifted_mean")

        def first_terms(rows):
            c = cols(rows)
            nc.vector.tensor_scalar_mul(out=first_x2[:, c], in0=first[:, c], scalar1=2.0)
            nc.vector.scalar_tensor_tensor(
                out=first_sq[:, c], in0=first[:, c], scalar=float(D), in1=first[:, c],
                op0=ALU.mult, op1=ALU.mult,
            )

        def norm_of_h(rows):
            c = cols(rows)
            nc.vector.tensor_add(out=h_sq_a[:, c], in0=shifted_sq[:, c], in1=first_sq[:, c])
            nc.vector.tensor_mul(out=h_sq_b[:, c], in0=shifted_sum[:, c], in1=first_x2[:, c])
            nc.vector.tensor_add(out=h_sq[:, c], in0=h_sq_a[:, c], in1=h_sq_b[:, c])
            power(h_norm, h_sq, half, rows)
            nc.gpsimd.tensor_scalar_min(out=h_clip[:, c], in0=h_norm[:, c], scalar1=BOUND)
            nc.vector.tensor_scalar_mul(
                out=shifted_mean[:, c], in0=shifted_sum[:, c], scalar1=1.0 / D
            )

        centred = per_tile([P, D], F32, "centred")

        def centre(rows):
            for i in rows:
                nc.vector.scalar_tensor_tensor(
                    out=centred[i][:], in0=shifted[i][:], scalar=shifted_mean[:, i : i + 1],
                    in1=gamma_bc[:], op0=ALU.subtract, op1=ALU.mult,
                )

        mean_part = row_numbers("mean_part")
        dev_sq = row_numbers("dev_sq")
        eps_h_sq = row_numbers("eps_h_sq")
        quarter_var = row_numbers("quarter_var")

        def variance(rows):
            c = cols(rows)
            nc.vector.tensor_mul(
                out=mean_part[:, c], in0=shifted_sum[:, c], in1=shifted_mean[:, c]
            )
            nc.vector.tensor_sub(out=dev_sq[:, c], in0=shifted_sq[:, c], in1=mean_part[:, c])
            nc.vector.tensor_scalar(
                out=eps_h_sq[:, c], in0=h_sq[:, c], scalar1=NORM_MIN_SQ, scalar2=LN_EPS,
                op0=ALU.max, op1=ALU.mult,
            )
            nc.vector.tensor_scalar_mul(out=quarter_var[:, c], in0=dev_sq[:, c], scalar1=0.25 / D)

        ln_up = row_numbers("ln_up")
        ln_dn = row_numbers("ln_dn")

        def log_of_h(rows):
            c = cols(rows)
            nc.scalar.activation(
                out=ln_up[:, c], in_=h_clip[:, c], func=ACT.Ln, bias=1.0, scale=1.0
            )
            nc.scalar.activation(
                out=ln_dn[:, c], in_=h_clip[:, c], func=ACT.Ln, bias=1.0, scale=-1.0
            )

        theta2 = row_numbers("theta2")
        theta2_sq = row_numbers("theta2_sq")
        factor_arg = row_numbers("factor_arg")
        factor_rsqrt = row_numbers("factor_rsqrt")
        ln_factor = row_numbers("ln_factor")

        def layer_norm_factor_argument(rows):
            c = cols(rows)
            for i in rows:
                nc.scalar.activation(
                    out=theta2_sq[:, i : i + 1], in_=ln_dn[:, i : i + 1], func=ACT.Square,
                    scale=-1.0, bias=ln_up[:, i : i + 1],
                )
            for i in rows:
                nc.scalar.activation(
                    out=factor_arg[:, i : i + 1], in_=theta2_sq[:, i : i + 1], func=ACT.Identity,
                    scale=quarter_var[:, i : i + 1], bias=eps_h_sq[:, i : i + 1],
                )
            power(factor_rsqrt, factor_arg, neg_half, rows)
            nc.vector.tensor_sub(out=theta2[:, c], in0=ln_up[:, c], in1=ln_dn[:, c])

        def layer_norm_factor(rows):
            c = cols(rows)
            nc.vector.scalar_tensor_tensor(
                out=ln_factor[:, c], in0=theta2[:, c], scalar=0.5, in1=factor_rsqrt[:, c],
                op0=ALU.mult, op1=ALU.mult,
            )

        x = per_tile([P, D], F32, "x")
        x_sq = row_numbers("x_sq")
        x_rnorm = row_numbers("x_rnorm")

        def layer_norm(rows):
            for i in rows:
                nc.vector.scalar_tensor_tensor(
                    out=x[i][:], in0=centred[i][:], scalar=ln_factor[:, i : i + 1],
                    in1=beta_bc[:], op0=ALU.mult, op1=ALU.add,
                )
                square_sum(x[i][:], x_sq[:, i : i + 1])

        bias_sq = one_number("bias_sq")
        bias_sq_clip = one_number("bias_sq_clip")
        bias_norm = one_number("bias_norm")
        bias_tanh = one_number("bias_tanh")
        bias_rnorm = one_number("bias_rnorm")
        y_scale = one_number("y_scale")
        neg_y_scale = one_number("neg_y_scale")
        y_sq = one_number("y_sq")
        one_plus_y_sq = one_number("one_plus_y_sq")

        def bias_square_sum():
            square_sum(bias_bc[:], bias_sq[:])
            load_table(ACT.Tanh, "table_tanh_1")

        def norm_of_bias():
            nc.vector.tensor_scalar_max(out=bias_sq_clip[:], in0=bias_sq[:], scalar1=NORM_MIN_SQ)
            nc.gpsimd.tensor_tensor(
                out=bias_norm[:], in0=bias_sq_clip[:], in1=half[:, 0:1], op=ALU.pow
            )

        def tanh_of_bias():
            nc.scalar.activation(out=bias_tanh[:], in_=bias_norm[:], func=ACT.Tanh)

        def bias_point():
            nc.vector.reciprocal(out=bias_rnorm[:], in_=bias_norm[:])
            nc.vector.tensor_mul(out=y_scale[:], in0=bias_tanh[:], in1=bias_rnorm[:])
            nc.vector.tensor_scalar_mul(out=neg_y_scale[:], in0=y_scale[:], scalar1=-1.0)
            nc.vector.tensor_scalar(
                out=y_sq[:], in0=bias_sq[:], scalar1=y_scale[:], scalar2=y_scale[:],
                op0=ALU.mult, op1=ALU.mult,
            )
            nc.vector.tensor_scalar_add(out=one_plus_y_sq[:], in0=y_sq[:], scalar1=1.0)

        w_t = [psum_tr.tile([P, 2, PACK, P], BF16, name="w_t%d" % b, tag="tr") for b in range(2)]
        w_grouped = keep.tile([P, D, PACK], BF16, name="w_grouped", align_bytes=64)
        w_codes = keep.tile([P, D], U32, name="w_codes", align_bytes=64)
        w_scales = keep.tile([P, D], U8, name="w_scales", align_bytes=64)

        def transpose_weight():
            for b in range(2):
                for a in range(2):
                    for t in range(PACK):
                        nc.tensor.transpose(
                            out=w_t[b][:, a, t, :],
                            in_=w_sb[:, 2 * b + a, t * P : (t + 1) * P],
                            identity=ident[:],
                        )

        def regroup_weight(b):
            nc.scalar.copy(
                out=w_grouped[:, 2 * b * P : 2 * (b + 1) * P, :].rearrange(
                    "p (a r) t -> p a r t", a=2
                ),
                in_=w_t[b][:].rearrange("p a t r -> p a r t"),
            )

        def quantise_weight():
            nc.vector.quantize_mx(
                out=w_codes[:].bitcast(FP8X4),
                scales=w_scales[:],
                in_=w_grouped[:].rearrange("p o t -> p (o t)"),
            )

        shrink = row_numbers("shrink")
        u = per_tile([P, D], BF16, "u")
        u_t = {}
        u_grouped = per_tile([P, P, PACK], BF16, "u_grouped")
        u_codes = per_tile([P, P], U32, "u_codes")
        u_scales = per_tile([P, P], U8, "u_scales")
        xt = [psum_xt.tile([P, D], F32, name="xt%d" % i) for i in range(TILES)]
        xt_sq = row_numbers("xt_sq")
        xt_y = row_numbers("xt_y")
        xt_norm = row_numbers("xt_norm")

        def shrink_factor(rows):
            c = cols(rows)
            power(x_rnorm, x_sq, neg_half, rows)
            nc.vector.tensor_scalar(
                out=shrink[:, c], in0=x_rnorm[:, c], scalar1=ARTANH_BOUND, scalar2=1.0,
                op0=ALU.mult, op1=ALU.min,
            )

        def make_u(rows):
            for i in rows:
                nc.vector.tensor_scalar_mul(out=u[i][:], in0=x[i][:], scalar1=shrink[:, i : i + 1])
                u_t[i] = psum_tr.tile([P, PACK, P], BF16, name="u_t", tag="tr")
                for t in range(PACK):
                    nc.tensor.transpose(
                        out=u_t[i][:, t, :], in_=u[i][:, t * P : (t + 1) * P], identity=ident[:]
                    )

        def regroup_u(rows):
            for i in rows:
                nc.scalar.copy(out=u_grouped[i][:], in_=u_t[i][:].rearrange("p t r -> p r t"))

        def multiply(rows):
            for i in rows:
                nc.vector.quantize_mx(
                    out=u_codes[i][:].bitcast(FP8X4),
                    scales=u_scales[i][:],
                    in_=u_grouped[i][:].rearrange("p r t -> p (r t)"),
                )
                nc.tensor.matmul_mx(
                    out=xt[i][:],
                    lhsT=u_codes[i][:].bitcast(FP8X4),
                    lhsT_scale=u_scales[i][:],
                    rhs=w_codes[:].bitcast(FP8X4),
                    rhs_scale=w_scales[:],
                    start=True,
                    stop=True,
                )

        def row_sums(rows):
            for i in rows:
                square_sum(xt[i][:], xt_sq[:, i : i + 1])
                products = scrap.tile([P, D], F32, name="products")
                nc.vector.scalar_tensor_tensor(
                    out=products[:], in0=xt[i][:], scalar=y_scale[:], in1=bias_bc[:],
                    op0=ALU.mult, op1=ALU.mult, accum_out=xt_y[:, i : i + 1],
                )

        r_norm = row_numbers("r_norm")
        xt_norm_clip = row_numbers("xt_norm_clip")
        xt_rnorm = row_numbers("xt_rnorm")
        xt_y_unit2 = row_numbers("xt_y_unit2")

        def exp_map(rows):
            c = cols(rows)
            power(xt_norm, xt_sq, half, rows)
            nc.scalar.activation(out=r_norm[:, c], in_=xt_norm[:, c], func=ACT.Tanh)
            nc.vector.tensor_scalar_max(out=xt_norm_clip[:, c], in0=xt_norm[:, c], scalar1=NORM_MIN)
            nc.vector.reciprocal(out=xt_rnorm[:, c], in_=xt_norm_clip[:, c])
            nc.vector.scalar_tensor_tensor(
                out=xt_y_unit2[:, c], in0=xt_rnorm[:, c], scalar=2.0, in1=xt_y[:, c],
                op0=ALU.mult, op1=ALU.mult,
            )

        r_y2 = row_numbers("r_y2")
        rho = row_numbers("rho")
        r_sq = row_numbers("r_sq")
        y_coef = row_numbers("y_coef")
        xt_coef = row_numbers("xt_coef")
        xt_rcoef = row_numbers("xt_rcoef")
        bias_coef = row_numbers("bias_coef")
        den_m1 = row_numbers("den_m1")
        den = row_numbers("den")
        sum_sq = row_numbers("sum_sq")
        sum_den = row_numbers("sum_den")
        sum_den_rsqrt = row_numbers("sum_den_rsqrt")
        r2_norm = row_numbers("r2_norm")
        r2_clip = row_numbers("r2_clip")

        def moebius_coefficients(rows):
            c = cols(rows)
            nc.vector.tensor_mul(out=r_y2[:, c], in0=r_norm[:, c], in1=xt_y_unit2[:, c])
            nc.vector.tensor_mul(out=rho[:, c], in0=r_norm[:, c], in1=xt_rnorm[:, c])
            nc.vector.tensor_mul(out=r_sq[:, c], in0=r_norm[:, c], in1=r_norm[:, c])
            nc.vector.scalar_tensor_tensor(
                out=xt_coef[:, c], in0=r_y2[:, c], scalar=one_plus_y_sq[:], in1=rho[:, c],
                op0=ALU.add, op1=ALU.mult,
            )
            nc.vector.tensor_scalar(
                out=y_coef[:, c], in0=r_sq[:, c], scalar1=neg_y_scale[:], scalar2=y_scale[:],
                op0=ALU.mult, op1=ALU.add,
            )
            nc.vector.scalar_tensor_tensor(
                out=den_m1[:, c], in0=r_sq[:, c], scalar=y_sq[:], in1=r_y2[:, c],
                op0=ALU.mult, op1=ALU.add,
            )
            nc.vector.reciprocal(out=xt_rcoef[:, c], in_=xt_coef[:, c])
            nc.vector.scalar_tensor_tensor(
                out=sum_sq[:, c], in0=r_sq[:, c], scalar=y_sq[:], in1=r_y2[:, c],
                op0=ALU.add, op1=ALU.add,
            )
            nc.vector.tensor_scalar(
                out=den[:, c], in0=den_m1[:, c], scalar1=1.0, scalar2=NORM_MIN,
                op0=ALU.add, op1=ALU.max,
            )
            nc.vector.tensor_mul(out=bias_coef[:, c], in0=y_coef[:, c], in1=xt_rcoef[:, c])

        def norm_of_r2(rows):
            c = cols(rows)
            nc.vector.scalar_tensor_tensor(
                out=sum_den[:, c], in0=sum_sq[:, c], scalar=SUM_SQ_MIN, in1=den[:, c],
                op0=ALU.max, op1=ALU.mult,
            )
            power(sum_den_rsqrt, sum_den, neg_half, rows)
            nc.gpsimd.tensor_tensor(
                out=r2_norm[:, c], in0=sum_sq[:, c], in1=sum_den_rsqrt[:, c], op=ALU.mult
            )
            nc.gpsimd.tensor_scalar_min(out=r2_clip[:, c], in0=r2_norm[:, c], scalar1=BOUND)

        z = per_tile([P, D], F32, "z")
        relu_sq = keep.tile([P, 2, 8], F32, name="relu_sq")
        relu_norm = row_numbers("relu_norm")

        def direction(rows):
            for i in rows:
                nc.vector.scalar_tensor_tensor(
                    out=z[i][:], in0=bias_bc[:], scalar=bias_coef[:, i : i + 1], in1=xt[i][:],
                    op0=ALU.mult, op1=ALU.add,
                )

        def relu_square_sums_on_vector(rows):
            for i in rows:
                products = scrap.tile([P, D], F32, name="products")
                nc.vector.scalar_tensor_tensor(
                    out=products[:], in0=z[i][:], scalar=0.0, in1=z[i][:],
                    op0=ALU.max, op1=ALU.mult, accum_out=relu_sq[:, i // 2, i % 2 : i % 2 + 1],
                )

        def relu_square_sums_on_scalar(rows):
            for i in rows:
                relu_z = scrap.tile([P, D], F32, name="relu_z")
                nc.scalar.activation(out=relu_z[:], in_=z[i][:], func=ACT.Relu)
                square_sum(relu_z[:], relu_sq[:, i // 2, i % 2 : i % 2 + 1])

        ln_up2 = row_numbers("ln_up2")
        ln_dn2 = row_numbers("ln_dn2")
        z_unit = row_numbers("z_unit")
        artanh2 = row_numbers("artanh2")
        log_coef = row_numbers("log_coef")

        def log_of_r2(rows):
            c = cols(rows)
            nc.scalar.activation(
                out=ln_up2[:, c], in_=r2_clip[:, c], func=ACT.Ln, bias=1.0, scale=1.0
            )
            nc.scalar.activation(
                out=ln_dn2[:, c], in_=r2_clip[:, c], func=ACT.Ln, bias=1.0, scale=-1.0
            )

        def log_map_coefficient(rows):
            c = cols(rows)
            nc.vector.tensor_mul(out=z_unit[:, c], in0=xt_coef[:, c], in1=sum_den_rsqrt[:, c])
            nc.vector.tensor_sub(out=artanh2[:, c], in0=ln_up2[:, c], in1=ln_dn2[:, c])
            nc.vector.scalar_tensor_tensor(
                out=log_coef[:, c], in0=artanh2[:, c], scalar=0.5, in1=z_unit[:, c],
                op0=ALU.mult, op1=ALU.mult,
            )

        v_norm = row_numbers("v_norm")
        v_tanh = row_numbers("v_tanh")
        relu_norm_clip = row_numbers("relu_norm_clip")
        relu_rnorm = row_numbers("relu_rnorm")
        out_coef = row_numbers("out_coef")
        result = per_tile([P, D], F32, "result")

        def out_coefficient():
            nc.gpsimd.tensor_tensor(
                out=relu_norm[:].rearrange("p (a b) -> p a b", a=2),
                in0=relu_sq[:, :, 0:2],
                in1=half[:].rearrange("p (a b) -> p a b", a=2),
                op=ALU.pow,
            )
            nc.vector.scalar_tensor_tensor(
                out=v_norm[:], in0=relu_norm[:], scalar=NORM_MIN, in1=log_coef[:],
                op0=ALU.max, op1=ALU.mult,
            )
            nc.scalar.activation(out=v_tanh[:], in_=v_norm[:], func=ACT.Tanh)
            nc.vector.tensor_scalar_max(out=relu_norm_clip[:], in0=relu_norm[:], scalar1=NORM_MIN)
            nc.vector.reciprocal(out=relu_rnorm[:], in_=relu_norm_clip[:])
            nc.vector.tensor_mul(out=out_coef[:], in0=v_tanh[:], in1=relu_rnorm[:])

        def finish(rows):
            for i in rows:
                if i == TILES - 1:
                    nc.scalar.activation(
                        out=result[i][:], in_=z[i][:], func=ACT.Relu, scale=out_coef[:, i : i + 1]
                    )
                else:
                    nc.vector.tensor_scalar(
                        out=result[i][:], in0=z[i][:], scalar1=0.0, scalar2=out_coef[:, i : i + 1],
                        op0=ALU.max, op1=ALU.mult,
                    )
                nc.sync.dma_start(out=out[i * P : (i + 1) * P, :], in_=result[i][:])

        ALL = range(TILES)
        FIRST_PAIR = range(0, 2)
        LAST_PAIR = range(2, 4)

        transpose_weight()
        shifted_sums(range(0, TILES - 1))
        first_terms(ALL)
        shifted_sums(range(TILES - 1, TILES))
        norm_of_h(ALL)
        regroup_weight(0)
        centre(FIRST_PAIR)
        variance(ALL)
        log_of_h(ALL)
        layer_norm_factor_argument(ALL)
        centre(LAST_PAIR)
        bias_square_sum()
        norm_of_bias()
        tanh_of_bias()
        layer_norm_factor(ALL)
        layer_norm(ALL)
        regroup_weight(1)
        bias_point()
        for rows in (FIRST_PAIR, LAST_PAIR):
            shrink_factor(rows)
            make_u(rows)
        quantise_weight()
        regroup_u(ALL)
        multiply(ALL)
        row_sums(ALL)
        exp_map(ALL)
        moebius_coefficients(ALL)
        load_table(ACT.Ln, "table_ln_2")
        direction(range(0, 1))
        norm_of_r2(ALL)
        direction(range(1, TILES))
        relu_square_sums_on_scalar(FIRST_PAIR)
        log_of_r2(ALL)
        load_table(ACT.Tanh, "table_tanh_2")
        relu_square_sums_on_vector(LAST_PAIR)
        log_map_coefficient(ALL)
        out_coefficient()
        finish(ALL)
